import numpy as np
import ml_dtypes


def mxq(x, axis, fmt="e4m3"):
    dtype, down = {"e4m3": (ml_dtypes.float8_e4m3fn, 7), "e5m2": (ml_dtypes.float8_e5m2, 14)}[fmt]
    v = np.moveaxis(np.asarray(x, np.float32).astype(ml_dtypes.bfloat16).astype(np.float64), axis, -1)
    blocks = v.reshape(v.shape[:-1] + (-1, 32))
    amax = np.abs(blocks).max(-1, keepdims=True)
    byte = np.maximum(np.where(amax > 0, np.frexp(amax)[1] - 1 + 127, 0) - down, 1)
    scale = np.exp2(byte - 127.0)
    codes = (blocks / scale).astype(np.float32).astype(dtype).astype(np.float64)
    return np.moveaxis((codes * scale).reshape(v.shape), -1, axis)


WIDE = False


def mx_kscale(k):
    if not WIDE:
        return np.ones(k)
    levels = np.array([10, -10, 5, -5, 0])
    a = np.random.permutation(np.resize(levels, k // 512 * 4)).reshape(k // 512, 4)
    idx = np.arange(k)
    return np.exp2(a[idx // 512, idx % 128 // 32])


BF16 = ml_dtypes.bfloat16


def bf(x):
    return np.asarray(x, np.float32).astype(BF16)


def f64(x):
    return np.asarray(x).astype(np.float64)


E2M1 = np.array([0.0, 0.5, 1.0, 1.5, 2.0, 3.0, 4.0, 6.0, -0.0, -0.5, -1.0, -1.5, -2.0, -3.0, -4.0, -6.0])


def pack_weight(w, fmt):
    k, n = w.shape
    w = f64(bf(w)).reshape(k // 32, 32, n)
    amax = np.abs(w).max(1)
    if fmt == "e4m3":
        byte = np.frexp(amax)[1] - 1 + 127 - 7
    else:
        mant, ex = np.frexp(amax / 6.0)
        byte = np.where(mant > 0.5, ex, ex - 1) + 127
    byte = np.clip(np.where(amax > 0, byte, 1), 1, 254)
    scaled = (w * np.exp2(127.0 - byte)[:, None, :]).reshape(k, n).astype(np.float32)
    by_word = np.ascontiguousarray(scaled.reshape(k // 512, 128, 4, n).transpose(0, 1, 3, 2))
    if fmt == "e4m3":
        words = by_word.astype(ml_dtypes.float8_e4m3fn).view(np.uint8)
    else:
        c = by_word.astype(ml_dtypes.float4_e2m1fn).view(np.uint8) & 0xF
        words = c[..., 0::2] | (c[..., 1::2] << 4)
    return np.ascontiguousarray(words), np.ascontiguousarray(byte.astype(np.uint8).reshape(k // 512, 16, n))


def unpack_weight(words, scales, fmt):
    g, p, n, _ = words.shape
    if fmt == "e4m3":
        vals = np.ascontiguousarray(words).view(ml_dtypes.float8_e4m3fn).astype(np.float64)
    else:
        nib = np.empty((g, p, n, 4), np.uint8)
        nib[..., 0::2] = words & 0xF
        nib[..., 1::2] = words >> 4
        vals = E2M1[nib]
    vals = vals * np.repeat(np.exp2(scales.astype(np.float64) - 127.0), 8, axis=1)[..., None]
    return vals.transpose(0, 1, 3, 2).reshape(g * 512, n)


B, IN, M, OUT = 256, 16384, 512, 512
F = 2 * M
EPS = 1e-12
FMT = "e4m3"


def setup_inputs():
    s, t = mx_kscale(IN), mx_kscale(F)
    x = bf(np.random.standard_normal((B, IN)) * s)
    W1_words, W1_scales = pack_weight(np.random.standard_normal((IN, F)) / np.sqrt(IN) / s[:, None] * t, FMT)
    b1 = bf(np.random.standard_normal(F) * 0.1 * t)
    W2_words, W2_scales = pack_weight(np.random.standard_normal((F, M)) / np.sqrt(F) / t[:, None], FMT)
    b2 = bf(np.random.standard_normal(M) * 0.3)
    return {"x": x,
            "W1_words": W1_words,
            "W1_scales": W1_scales,
            "b1": b1,
            "W2_words": W2_words,
            "W2_scales": W2_scales,
            "b2": b2}


def reference(x, W1_words, W1_scales, b1, W2_words, W2_scales, b2):
    h = np.maximum((mxq(f64(x), 1, "e4m3") @ unpack_weight(W1_words, W1_scales, FMT)) + f64(b1), 0.0)
    v = (mxq(h, 1, "e4m3") @ unpack_weight(W2_words, W2_scales, FMT)) + f64(b2)
    norm = np.sqrt(np.sum(v * v, axis=-1, keepdims=True))
    return v / np.maximum(norm, EPS)

@@ -1,0 +1,291 @@
+from contextlib import ExitStack
+
+import concourse.mybir as mybir
+from concourse.masks import make_identity
+
+BF16 = mybir.dt.bfloat16
+F32 = mybir.dt.float32
+I32 = mybir.dt.int32
+U32 = mybir.dt.uint32
+U8 = mybir.dt.uint8
+FP8X4 = mybir.dt.float8_e4m3fn_x4
+ALU = mybir.AluOpType
+ACT = mybir.ActivationFunctionType
+
+B, IN, F, M = 256, 16384, 1024, 512
+EPS = 1e-12
+FLOPS = 2 * B * IN * F + 2 * B * F * M
+
+P = 128
+PACK = 4
+K_PASS = P * PACK
+N_PASS = 512
+B_TILES = B // P
+F_HALVES = F // N_PASS
+GROUPS = IN // K_PASS
+ROUND = 4
+ROUNDS = GROUPS // ROUND
+QUADRANTS = 4
+W2_LOAD_STEP = 4
+
+
+def tile_geometricmanifoldnetwork_pa_k_kernel(
+    tc, x, W1_words, W1_scales, b1, W2_words, W2_scales, b2, out
+):
+    nc = tc.nc
+
+    x_rows = x.rearrange("(t b) k -> b t k", b=P)
+    w1_word_rows = W1_words.rearrange("g p n t -> g p (n t)").bitcast(I32)
+    w1_scale_rows = W1_scales.bitcast(I32)
+    w2_word_rows = W2_words.rearrange("g p n t -> g p (n t)").bitcast(I32)
+    w2_scale_rows = W2_scales.bitcast(I32)
+
+    with ExitStack() as ctx:
+        const = ctx.enter_context(tc.tile_pool(name="const", bufs=1))
+        x_pool = ctx.enter_context(tc.tile_pool(name="x_pool", bufs=3))
+        sort_pool = ctx.enter_context(tc.tile_pool(name="sort_pool", bufs=2))
+        group_pool = ctx.enter_context(tc.tile_pool(name="group_pool", bufs=2))
+        xq_pool = ctx.enter_context(tc.tile_pool(name="xq_pool", bufs=3))
+        w_pool = ctx.enter_context(tc.tile_pool(name="w_pool", bufs=6))
+        tail = ctx.enter_context(tc.tile_pool(name="tail", bufs=1))
+        acc_pool = ctx.enter_context(tc.psum_pool(name="acc_pool", bufs=1))
+        work = ctx.enter_context(tc.psum_pool(name="work", bufs=4))
+        ctx.enter_context(tc.manual_schedule())
+
+        warm = const.tile([P, 1], F32)
+        nc.vector.memset(warm[:], 1.0)
+        nc.scalar.activation(out=warm[:], in_=warm[:], func=ACT.Sqrt)
+
+        ident_f32 = const.tile([P, P], F32)
+        make_identity(nc, ident_f32[:])
+        ident_bf16 = const.tile([P, P], BF16)
+        make_identity(nc, ident_bf16[:])
+
+        bias_rows = const.tile([P, F + M], BF16)
+        nc.vector.memset(bias_rows[:], 0.0)
+        ones = const.tile([P, P], BF16)
+        nc.vector.memset(ones[:], 1.0)
+        w1_planes = const.tile([P, ROUNDS * F], U8, align_bytes=64)
+        nc.vector.memset(w1_planes[:].bitcast(I32), 0)
+        w2_planes = const.tile([P, M], U8, align_bytes=64)
+        nc.vector.memset(w2_planes[:].bitcast(I32), 0)
+        w2_words = const.tile([P, F_HALVES, M], U32, align_bytes=64)
+
+        nc.scalar.dma_start(out=bias_rows[0:1, 0:F], in_=b1.rearrange("(o f) -> o f", o=1))
+        nc.scalar.dma_start(out=bias_rows[0:1, F : F + M], in_=b2.rearrange("(o f) -> o f", o=1))
+        b1_sorted = const.tile([P, F_HALVES, PACK, P], F32)
+        b2_spread = const.tile([P, M], F32)
+        for half in range(F_HALVES):
+            b1_bank = work.tile([P, N_PASS], F32, tag="work")
+            nc.tensor.matmul(
+                out=b1_bank[:],
+                lhsT=ones[:],
+                rhs=bias_rows[:, half * N_PASS : (half + 1) * N_PASS],
+                start=True,
+                stop=True,
+            )
+            nc.scalar.copy(
+                out=b1_sorted[:, half], in_=b1_bank[:].rearrange("b (q t) -> b t q", t=PACK)
+            )
+        b2_bank = work.tile([P, M], F32, tag="work")
+        nc.tensor.matmul(
+            out=b2_bank[:], lhsT=ones[:], rhs=bias_rows[:, F : F + M], start=True, stop=True
+        )
+        nc.scalar.copy(out=b2_spread[:], in_=b2_bank[:])
+
+        h_acc = {}
+        for bt in range(B_TILES):
+            for half in range(F_HALVES):
+                h_bank = acc_pool.tile([P, N_PASS], F32, name="h_acc_%d_%d" % (bt, half))
+                h_acc[(bt, half)] = h_bank
+
+        x_raw_of = {}
+        x_sorted_of = {}
+        x_codes_of = {}
+        x_scales_of = {}
+        w_words_of = {}
+
+        def load_x(r):
+            x_raw = x_pool.tile([P, B_TILES, ROUND * K_PASS], BF16)
+            nc.sync.dma_start(
+                out=x_raw[:], in_=x_rows[:, :, r * ROUND * K_PASS : (r + 1) * ROUND * K_PASS]
+            )
+            x_raw_of[r] = x_raw
+
+        def load_w(r):
+            groups = slice(r * ROUND, (r + 1) * ROUND)
+            for quadrant in range(QUADRANTS):
+                nc.sync.dma_start(
+                    out=w1_planes[
+                        32 * quadrant : 32 * quadrant + 4 * ROUND, r * F : (r + 1) * F
+                    ].bitcast(I32),
+                    in_=w1_scale_rows[groups, 4 * quadrant : 4 * quadrant + 4, :],
+                )
+            w_words = w_pool.tile([P, ROUND, F], U32, align_bytes=64)
+            step = 1 if r == ROUNDS - 1 else ROUND
+            for j in range(0, ROUND, step):
+                nc.sync.dma_start(
+                    out=w_words[:, j : j + step, :].bitcast(I32),
+                    in_=w1_word_rows[r * ROUND + j : r * ROUND + j + step].rearrange(
+                        "g p n -> p g n"
+                    ),
+                )
+            w_words_of[r] = w_words
+
+        def sort_words(r):
+            x_sorted = sort_pool.tile([P, B_TILES * ROUND, 2, P], F32)
+            nc.vector.tensor_copy(
+                out=x_sorted[:],
+                in_=x_raw_of[r][:].bitcast(F32).rearrange("b t (g q u) -> b (t g) u q", q=P, u=2),
+            )
+            x_sorted_of[r] = x_sorted
+
+        def transpose_and_quantise(r):
+            x_sorted = x_sorted_of[r]
+            grouped = group_pool.tile([P, ROUND * B * PACK], BF16, align_bytes=64)
+            grouped_words = grouped[:].bitcast(F32).rearrange("q (g b u) -> q g b u", g=ROUND, u=2)
+            for j in range(ROUND):
+                xt = work.tile([P, 2, B], F32, tag="work")
+                for u in range(2):
+                    for bt in range(B_TILES):
+                        nc.tensor.transpose(
+                            xt[:, u, bt * P : (bt + 1) * P],
+                            x_sorted[:, bt * ROUND + j, u, :],
+                            ident_f32[:],
+                        )
+                nc.scalar.copy(out=grouped_words[:, j], in_=xt[:].rearrange("q u b -> q b u"))
+            x_codes = xq_pool.tile([P, ROUND * B], U32, align_bytes=64)
+            x_scales = xq_pool.tile([P, ROUND * B], U8, align_bytes=64)
+            nc.vector.quantize_mx(
+                out=x_codes[:].bitcast(FP8X4), scales=x_scales[:], in_=grouped[:]
+            )
+            x_codes_of[r] = x_codes
+            x_scales_of[r] = x_scales
+
+        def multiply(r):
+            for j in range(ROUND):
+                group = r * ROUND + j
+                for half in range(F_HALVES):
+                    for bt in range(B_TILES):
+                        rows = slice(j * B + bt * P, j * B + (bt + 1) * P)
+                        nc.tensor.matmul_mx(
+                            out=h_acc[(bt, half)][:],
+                            lhsT=x_codes_of[r][:, rows].bitcast(FP8X4),
+                            lhsT_scale=x_scales_of[r][:, rows],
+                            rhs=w_words_of[r][
+                                :, j, half * N_PASS : (half + 1) * N_PASS
+                            ].bitcast(FP8X4),
+                            rhs_scale=w1_planes[
+                                4 * j : P, r * F + half * N_PASS : r * F + (half + 1) * N_PASS
+                            ],
+                            start=(group == 0),
+                            stop=(group == GROUPS - 1),
+                        )
+
+        def load_w2():
+            for quadrant in range(QUADRANTS):
+                nc.sync.dma_start(
+                    out=w2_planes[32 * quadrant : 32 * quadrant + 4 * F_HALVES, :].bitcast(I32),
+                    in_=w2_scale_rows[:, 4 * quadrant : 4 * quadrant + 4, :],
+                )
+            nc.sync.dma_start(
+                out=w2_words[:].bitcast(I32), in_=w2_word_rows.rearrange("g p n -> p g n")
+            )
+
+        def if_round(stage, r):
+            if 0 <= r < ROUNDS:
+                stage(r)
+
+        for s in range(ROUNDS + 3):
+            if_round(load_x, s)
+            if_round(load_w, s - 2)
+            if s == W2_LOAD_STEP:
+                load_w2()
+            if_round(sort_words, s - 1)
+            if_round(transpose_and_quantise, s - 2)
+            if_round(multiply, s - 3)
+
+        h_sorted = tail.tile([P, B_TILES, F_HALVES, PACK, P], BF16)
+        for half in range(F_HALVES):
+            for bt in range(B_TILES):
+                nc.vector.tensor_tensor(
+                    out=h_sorted[:, bt, half],
+                    in0=h_acc[(bt, half)][:].rearrange("b (q t) -> b t q", t=PACK),
+                    in1=b1_sorted[:, half],
+                    op=ALU.add,
+                )
+
+        h_grouped = tail.tile([P, F_HALVES, B, PACK], BF16, align_bytes=64)
+        h_codes = tail.tile([P, F_HALVES * B], U32, align_bytes=64)
+        h_scales = tail.tile([P, F_HALVES * B], U8, align_bytes=64)
+        ht_of = {}
+
+        def transpose_h(half):
+            for bt in range(B_TILES):
+                ht = work.tile([P, PACK, P], BF16, tag="work")
+                for t in range(PACK):
+                    nc.tensor.transpose(ht[:, t, :], h_sorted[:, bt, half, t, :], ident_bf16[:])
+                ht_of[(bt, half)] = ht
+
+        def relu_and_quantise_h(half):
+            nc.scalar.activation(
+                out=h_grouped[:, half, 0:P, :],
+                in_=ht_of[(0, half)][:].rearrange("q t b -> q b t"),
+                func=ACT.Relu,
+            )
+            nc.vector.tensor_scalar_max(
+                out=h_grouped[:, half, P:B, :],
+                in0=ht_of[(1, half)][:].rearrange("q t b -> q b t"),
+                scalar1=0.0,
+            )
+            nc.vector.quantize_mx(
+                out=h_codes[:, half * B : (half + 1) * B].bitcast(FP8X4),
+                scales=h_scales[:, half * B : (half + 1) * B],
+                in_=h_grouped[:, half].rearrange("q b t -> q (b t)"),
+            )
+
+        transpose_h(0)
+        transpose_h(1)
+        relu_and_quantise_h(0)
+        relu_and_quantise_h(1)
+
+        v_acc = {}
+        for bt in range(B_TILES):
+            v_bank = work.tile([P, M], F32, tag="work")
+            v_acc[bt] = v_bank
+        for half in range(F_HALVES):
+            for bt in range(B_TILES):
+                rows = slice(half * B + bt * P, half * B + (bt + 1) * P)
+                nc.tensor.matmul_mx(
+                    out=v_acc[bt][:],
+                    lhsT=h_codes[:, rows].bitcast(FP8X4),
+                    lhsT_scale=h_scales[:, rows],
+                    rhs=w2_words[:, half, :].bitcast(FP8X4),
+                    rhs_scale=w2_planes[4 * half : P, :],
+                    start=(half == 0),
+                    stop=(half == F_HALVES - 1),
+                )
+
+        v = tail.tile([P, B_TILES, M], F32)
+        squares = tail.tile([P, B_TILES, M], F32)
+        sum_squares = tail.tile([P, B_TILES], F32)
+        clamped = tail.tile([P, B_TILES], F32)
+        norm = tail.tile([P, B_TILES], F32)
+        inv_norm = tail.tile([P, B_TILES], F32)
+        unit = tail.tile([P, B_TILES, M], F32)
+        for bt in range(B_TILES):
+            nc.vector.tensor_tensor(out=v[:, bt], in0=v_acc[bt][:], in1=b2_spread[:], op=ALU.add)
+            nc.scalar.activation(
+                out=squares[:, bt],
+                in_=v[:, bt],
+                func=ACT.Square,
+                accum_out=sum_squares[:, bt : bt + 1],
+            )
+        nc.vector.tensor_scalar_max(out=clamped[:], in0=sum_squares[:], scalar1=EPS * EPS)
+        nc.scalar.activation(out=norm[:], in_=clamped[:], func=ACT.Sqrt)
+        nc.vector.reciprocal(out=inv_norm[:], in_=norm[:])
+        for bt in range(B_TILES):
+            nc.vector.tensor_scalar_mul(
+                out=unit[:, bt], in0=v[:, bt], scalar1=inv_norm[:, bt : bt + 1]
+            )
+            nc.sync.dma_start(out=out[bt * P : (bt + 1) * P, :], in_=unit[:, bt])

@@ -26,7 +26,8 @@ GROUPS = IN // K_PASS
 ROUND = 4
 ROUNDS = GROUPS // ROUND
 QUADRANTS = 4
-W2_LOAD_STEP = 4
+X_BUFS = 4
+W_BUFS = 5
 
 
 def tile_geometricmanifoldnetwork_pa_k_kernel(
@@ -42,11 +43,9 @@ def tile_geometricmanifoldnetwork_pa_k_kernel(
 
     with ExitStack() as ctx:
         const = ctx.enter_context(tc.tile_pool(name="const", bufs=1))
-        x_pool = ctx.enter_context(tc.tile_pool(name="x_pool", bufs=3))
-        sort_pool = ctx.enter_context(tc.tile_pool(name="sort_pool", bufs=2))
+        x_pool = ctx.enter_context(tc.tile_pool(name="x_pool", bufs=X_BUFS))
         group_pool = ctx.enter_context(tc.tile_pool(name="group_pool", bufs=2))
-        xq_pool = ctx.enter_context(tc.tile_pool(name="xq_pool", bufs=3))
-        w_pool = ctx.enter_context(tc.tile_pool(name="w_pool", bufs=6))
+        w_pool = ctx.enter_context(tc.tile_pool(name="w_pool", bufs=W_BUFS))
         tail = ctx.enter_context(tc.tile_pool(name="tail", bufs=1))
         acc_pool = ctx.enter_context(tc.psum_pool(name="acc_pool", bufs=1))
         work = ctx.enter_context(tc.psum_pool(name="work", bufs=4))
@@ -65,6 +64,7 @@ def tile_geometricmanifoldnetwork_pa_k_kernel(
         nc.vector.memset(bias_rows[:], 0.0)
         ones = const.tile([P, P], BF16)
         nc.vector.memset(ones[:], 1.0)
+
         w1_planes = const.tile([P, ROUNDS * F], U8, align_bytes=64)
         nc.vector.memset(w1_planes[:].bitcast(I32), 0)
         w2_planes = const.tile([P, M], U8, align_bytes=64)
@@ -100,10 +100,9 @@ def tile_geometricmanifoldnetwork_pa_k_kernel(
                 h_acc[(bt, half)] = h_bank
 
         x_raw_of = {}
-        x_sorted_of = {}
-        x_codes_of = {}
-        x_scales_of = {}
         w_words_of = {}
+        x_codes = const.tile([P, GROUPS * B], U32, align_bytes=64)
+        x_scales = const.tile([P, GROUPS * B], U8, align_bytes=64)
 
         def load_x(r):
             x_raw = x_pool.tile([P, B_TILES, ROUND * K_PASS], BF16)
@@ -111,16 +110,17 @@ def tile_geometricmanifoldnetwork_pa_k_kernel(
                 out=x_raw[:], in_=x_rows[:, :, r * ROUND * K_PASS : (r + 1) * ROUND * K_PASS]
             )
             x_raw_of[r] = x_raw
-
-        def load_w(r):
-            groups = slice(r * ROUND, (r + 1) * ROUND)
             for quadrant in range(QUADRANTS):
                 nc.sync.dma_start(
                     out=w1_planes[
                         32 * quadrant : 32 * quadrant + 4 * ROUND, r * F : (r + 1) * F
                     ].bitcast(I32),
-                    in_=w1_scale_rows[groups, 4 * quadrant : 4 * quadrant + 4, :],
+                    in_=w1_scale_rows[
+                        r * ROUND : (r + 1) * ROUND, 4 * quadrant : 4 * quadrant + 4, :
+                    ],
                 )
+
+        def load_w(r):
             w_words = w_pool.tile([P, ROUND, F], U32, align_bytes=64)
             step = 1 if r == ROUNDS - 1 else ROUND
             for j in range(0, ROUND, step):
@@ -132,16 +132,8 @@ def tile_geometricmanifoldnetwork_pa_k_kernel(
                 )
             w_words_of[r] = w_words
 
-        def sort_words(r):
-            x_sorted = sort_pool.tile([P, B_TILES * ROUND, 2, P], F32)
-            nc.vector.tensor_copy(
-                out=x_sorted[:],
-                in_=x_raw_of[r][:].bitcast(F32).rearrange("b t (g q u) -> b (t g) u q", q=P, u=2),
-            )
-            x_sorted_of[r] = x_sorted
-
         def transpose_and_quantise(r):
-            x_sorted = x_sorted_of[r]
+            x_words = x_raw_of[r][:].bitcast(F32)
             grouped = group_pool.tile([P, ROUND * B * PACK], BF16, align_bytes=64)
             grouped_words = grouped[:].bitcast(F32).rearrange("q (g b u) -> q g b u", g=ROUND, u=2)
             for j in range(ROUND):
@@ -150,28 +142,30 @@ def tile_geometricmanifoldnetwork_pa_k_kernel(
                     for bt in range(B_TILES):
                         nc.tensor.transpose(
                             xt[:, u, bt * P : (bt + 1) * P],
-                            x_sorted[:, bt * ROUND + j, u, :],
+                            x_words[:, bt, j * 2 * P + u : (j + 1) * 2 * P : 2],
                             ident_f32[:],
                         )
-                nc.scalar.copy(out=grouped_words[:, j], in_=xt[:].rearrange("q u b -> q b u"))
-            x_codes = xq_pool.tile([P, ROUND * B], U32, align_bytes=64)
-            x_scales = xq_pool.tile([P, ROUND * B], U8, align_bytes=64)
+                if j < ROUND - 1:
+                    nc.scalar.copy(out=grouped_words[:, j], in_=xt[:].rearrange("q u b -> q b u"))
+                else:
+                    nc.vector.tensor_copy(
+                        out=grouped_words[:, j], in_=xt[:].rearrange("q u b -> q b u")
+                    )
+            columns = slice(r * ROUND * B, (r + 1) * ROUND * B)
             nc.vector.quantize_mx(
-                out=x_codes[:].bitcast(FP8X4), scales=x_scales[:], in_=grouped[:]
+                out=x_codes[:, columns].bitcast(FP8X4), scales=x_scales[:, columns], in_=grouped[:]
             )
-            x_codes_of[r] = x_codes
-            x_scales_of[r] = x_scales
 
         def multiply(r):
             for j in range(ROUND):
                 group = r * ROUND + j
                 for half in range(F_HALVES):
                     for bt in range(B_TILES):
-                        rows = slice(j * B + bt * P, j * B + (bt + 1) * P)
+                        rows = slice(group * B + bt * P, group * B + (bt + 1) * P)
                         nc.tensor.matmul_mx(
                             out=h_acc[(bt, half)][:],
-                            lhsT=x_codes_of[r][:, rows].bitcast(FP8X4),
-                            lhsT_scale=x_scales_of[r][:, rows],
+                            lhsT=x_codes[:, rows].bitcast(FP8X4),
+                            lhsT_scale=x_scales[:, rows],
                             rhs=w_words_of[r][
                                 :, j, half * N_PASS : (half + 1) * N_PASS
                             ].bitcast(FP8X4),
@@ -192,18 +186,19 @@ def tile_geometricmanifoldnetwork_pa_k_kernel(
                 out=w2_words[:].bitcast(I32), in_=w2_word_rows.rearrange("g p n -> p g n")
             )
 
-        def if_round(stage, r):
-            if 0 <= r < ROUNDS:
-                stage(r)
-
-        for s in range(ROUNDS + 3):
-            if_round(load_x, s)
-            if_round(load_w, s - 2)
-            if s == W2_LOAD_STEP:
-                load_w2()
-            if_round(sort_words, s - 1)
-            if_round(transpose_and_quantise, s - 2)
-            if_round(multiply, s - 3)
+        for r in range(X_BUFS):
+            load_x(r)
+        for r in range(ROUNDS):
+            transpose_and_quantise(r)
+            if r + X_BUFS < ROUNDS:
+                load_x(r + X_BUFS)
+        for r in range(W_BUFS):
+            load_w(r)
+        load_w2()
+        for r in range(ROUNDS):
+            multiply(r)
+            if r + W_BUFS < ROUNDS:
+                load_w(r + W_BUFS)
 
         h_sorted = tail.tile([P, B_TILES, F_HALVES, PACK, P], BF16)
         for half in range(F_HALVES):

@@ -37,9 +37,9 @@ def tile_geometricmanifoldnetwork_pa_k_kernel(
 
     x_rows = x.rearrange("(t b) k -> b t k", b=P)
     w1_word_rows = W1_words.rearrange("g p n t -> g p (n t)").bitcast(I32)
-    w1_scale_rows = W1_scales.bitcast(I32)
+    w1_scale_rows = W1_scales.bitcast(F32)
     w2_word_rows = W2_words.rearrange("g p n t -> g p (n t)").bitcast(I32)
-    w2_scale_rows = W2_scales.bitcast(I32)
+    w2_scale_rows = W2_scales.bitcast(F32)
 
     with ExitStack() as ctx:
         const = ctx.enter_context(tc.tile_pool(name="const", bufs=1))
@@ -70,6 +70,21 @@ def tile_geometricmanifoldnetwork_pa_k_kernel(
         w2_planes = const.tile([P, M], U8, align_bytes=64)
         nc.vector.memset(w2_planes[:].bitcast(I32), 0)
         w2_words = const.tile([P, F_HALVES, M], U32, align_bytes=64)
+        for r in range(ROUNDS):
+            for quadrant in range(QUADRANTS):
+                nc.gpsimd.dma_start(
+                    out=w1_planes[
+                        32 * quadrant : 32 * quadrant + 4 * ROUND, r * F : (r + 1) * F
+                    ].bitcast(F32),
+                    in_=w1_scale_rows[
+                        r * ROUND : (r + 1) * ROUND, 4 * quadrant : 4 * quadrant + 4, :
+                    ],
+                )
+        for quadrant in range(QUADRANTS):
+            nc.gpsimd.dma_start(
+                out=w2_planes[32 * quadrant : 32 * quadrant + 4 * F_HALVES, :].bitcast(F32),
+                in_=w2_scale_rows[:, 4 * quadrant : 4 * quadrant + 4, :],
+            )
 
         nc.scalar.dma_start(out=bias_rows[0:1, 0:F], in_=b1.rearrange("(o f) -> o f", o=1))
         nc.scalar.dma_start(out=bias_rows[0:1, F : F + M], in_=b2.rearrange("(o f) -> o f", o=1))
@@ -110,15 +125,6 @@ def tile_geometricmanifoldnetwork_pa_k_kernel(
                 out=x_raw[:], in_=x_rows[:, :, r * ROUND * K_PASS : (r + 1) * ROUND * K_PASS]
             )
             x_raw_of[r] = x_raw
-            for quadrant in range(QUADRANTS):
-                nc.sync.dma_start(
-                    out=w1_planes[
-                        32 * quadrant : 32 * quadrant + 4 * ROUND, r * F : (r + 1) * F
-                    ].bitcast(I32),
-                    in_=w1_scale_rows[
-                        r * ROUND : (r + 1) * ROUND, 4 * quadrant : 4 * quadrant + 4, :
-                    ],
-                )
 
         def load_w(r):
             w_words = w_pool.tile([P, ROUND, F], U32, align_bytes=64)
@@ -176,16 +182,6 @@ def tile_geometricmanifoldnetwork_pa_k_kernel(
                             stop=(group == GROUPS - 1),
                         )
 
-        def load_w2():
-            for quadrant in range(QUADRANTS):
-                nc.sync.dma_start(
-                    out=w2_planes[32 * quadrant : 32 * quadrant + 4 * F_HALVES, :].bitcast(I32),
-                    in_=w2_scale_rows[:, 4 * quadrant : 4 * quadrant + 4, :],
-                )
-            nc.sync.dma_start(
-                out=w2_words[:].bitcast(I32), in_=w2_word_rows.rearrange("g p n -> p g n")
-            )
-
         for r in range(X_BUFS):
             load_x(r)
         for r in range(ROUNDS):
@@ -194,7 +190,9 @@ def tile_geometricmanifoldnetwork_pa_k_kernel(
                 load_x(r + X_BUFS)
         for r in range(W_BUFS):
             load_w(r)
-        load_w2()
+        nc.sync.dma_start(
+            out=w2_words[:].bitcast(I32), in_=w2_word_rows.rearrange("g p n -> p g n")
+        )
         for r in range(ROUNDS):
             multiply(r)
             if r + W_BUFS < ROUNDS:

@@ -26,8 +26,7 @@ GROUPS = IN // K_PASS
 ROUND = 4
 ROUNDS = GROUPS // ROUND
 QUADRANTS = 4
-X_BUFS = 4
-W_BUFS = 5
+W2_LOAD_STEP = 4
 
 
 def tile_geometricmanifoldnetwork_pa_k_kernel(
@@ -43,9 +42,11 @@ def tile_geometricmanifoldnetwork_pa_k_kernel(
 
     with ExitStack() as ctx:
         const = ctx.enter_context(tc.tile_pool(name="const", bufs=1))
-        x_pool = ctx.enter_context(tc.tile_pool(name="x_pool", bufs=X_BUFS))
+        x_pool = ctx.enter_context(tc.tile_pool(name="x_pool", bufs=3))
+        sort_pool = ctx.enter_context(tc.tile_pool(name="sort_pool", bufs=2))
         group_pool = ctx.enter_context(tc.tile_pool(name="group_pool", bufs=2))
-        w_pool = ctx.enter_context(tc.tile_pool(name="w_pool", bufs=W_BUFS))
+        xq_pool = ctx.enter_context(tc.tile_pool(name="xq_pool", bufs=3))
+        w_pool = ctx.enter_context(tc.tile_pool(name="w_pool", bufs=6))
         tail = ctx.enter_context(tc.tile_pool(name="tail", bufs=1))
         acc_pool = ctx.enter_context(tc.psum_pool(name="acc_pool", bufs=1))
         work = ctx.enter_context(tc.psum_pool(name="work", bufs=4))
@@ -115,9 +116,10 @@ def tile_geometricmanifoldnetwork_pa_k_kernel(
                 h_acc[(bt, half)] = h_bank
 
         x_raw_of = {}
+        x_sorted_of = {}
+        x_codes_of = {}
+        x_scales_of = {}
         w_words_of = {}
-        x_codes = const.tile([P, GROUPS * B], U32, align_bytes=64)
-        x_scales = const.tile([P, GROUPS * B], U8, align_bytes=64)
 
         def load_x(r):
             x_raw = x_pool.tile([P, B_TILES, ROUND * K_PASS], BF16)
@@ -138,8 +140,16 @@ def tile_geometricmanifoldnetwork_pa_k_kernel(
                 )
             w_words_of[r] = w_words
 
+        def sort_words(r):
+            x_sorted = sort_pool.tile([P, B_TILES * ROUND, 2, P], F32)
+            nc.vector.tensor_copy(
+                out=x_sorted[:],
+                in_=x_raw_of[r][:].bitcast(F32).rearrange("b t (g q u) -> b (t g) u q", q=P, u=2),
+            )
+            x_sorted_of[r] = x_sorted
+
         def transpose_and_quantise(r):
-            x_words = x_raw_of[r][:].bitcast(F32)
+            x_sorted = x_sorted_of[r]
             grouped = group_pool.tile([P, ROUND * B * PACK], BF16, align_bytes=64)
             grouped_words = grouped[:].bitcast(F32).rearrange("q (g b u) -> q g b u", g=ROUND, u=2)
             for j in range(ROUND):
@@ -148,30 +158,28 @@ def tile_geometricmanifoldnetwork_pa_k_kernel(
                     for bt in range(B_TILES):
                         nc.tensor.transpose(
                             xt[:, u, bt * P : (bt + 1) * P],
-                            x_words[:, bt, j * 2 * P + u : (j + 1) * 2 * P : 2],
+                            x_sorted[:, bt * ROUND + j, u, :],
                             ident_f32[:],
                         )
-                if j < ROUND - 1:
-                    nc.scalar.copy(out=grouped_words[:, j], in_=xt[:].rearrange("q u b -> q b u"))
-                else:
-                    nc.vector.tensor_copy(
-                        out=grouped_words[:, j], in_=xt[:].rearrange("q u b -> q b u")
-                    )
-            columns = slice(r * ROUND * B, (r + 1) * ROUND * B)
+                nc.scalar.copy(out=grouped_words[:, j], in_=xt[:].rearrange("q u b -> q b u"))
+            x_codes = xq_pool.tile([P, ROUND * B], U32, align_bytes=64)
+            x_scales = xq_pool.tile([P, ROUND * B], U8, align_bytes=64)
             nc.vector.quantize_mx(
-                out=x_codes[:, columns].bitcast(FP8X4), scales=x_scales[:, columns], in_=grouped[:]
+                out=x_codes[:].bitcast(FP8X4), scales=x_scales[:], in_=grouped[:]
             )
+            x_codes_of[r] = x_codes
+            x_scales_of[r] = x_scales
 
         def multiply(r):
             for j in range(ROUND):
                 group = r * ROUND + j
                 for half in range(F_HALVES):
                     for bt in range(B_TILES):
-                        rows = slice(group * B + bt * P, group * B + (bt + 1) * P)
+                        rows = slice(j * B + bt * P, j * B + (bt + 1) * P)
                         nc.tensor.matmul_mx(
                             out=h_acc[(bt, half)][:],
-                            lhsT=x_codes[:, rows].bitcast(FP8X4),
-                            lhsT_scale=x_scales[:, rows],
+                            lhsT=x_codes_of[r][:, rows].bitcast(FP8X4),
+                            lhsT_scale=x_scales_of[r][:, rows],
                             rhs=w_words_of[r][
                                 :, j, half * N_PASS : (half + 1) * N_PASS
                             ].bitcast(FP8X4),
@@ -182,21 +190,23 @@ def tile_geometricmanifoldnetwork_pa_k_kernel(
                             stop=(group == GROUPS - 1),
                         )
 
-        for r in range(X_BUFS):
-            load_x(r)
-        for r in range(ROUNDS):
-            transpose_and_quantise(r)
-            if r + X_BUFS < ROUNDS:
-                load_x(r + X_BUFS)
-        for r in range(W_BUFS):
-            load_w(r)
-        nc.sync.dma_start(
-            out=w2_words[:].bitcast(I32), in_=w2_word_rows.rearrange("g p n -> p g n")
-        )
-        for r in range(ROUNDS):
-            multiply(r)
-            if r + W_BUFS < ROUNDS:
-                load_w(r + W_BUFS)
+        def load_w2():
+            nc.sync.dma_start(
+                out=w2_words[:].bitcast(I32), in_=w2_word_rows.rearrange("g p n -> p g n")
+            )
+
+        def if_round(stage, r):
+            if 0 <= r < ROUNDS:
+                stage(r)
+
+        for s in range(ROUNDS + 3):
+            if_round(load_w, s - 2)
+            if_round(load_x, s)
+            if s == W2_LOAD_STEP:
+                load_w2()
+            if_round(sort_words, s - 1)
+            if_round(transpose_and_quantise, s - 2)
+            if_round(multiply, s - 3)
 
         h_sorted = tail.tile([P, B_TILES, F_HALVES, PACK, P], BF16)
         for half in range(F_HALVES):

@@ -23,10 +23,18 @@ N_PASS = 512
 B_TILES = B // P
 F_HALVES = F // N_PASS
 GROUPS = IN // K_PASS
+QUADRANTS = 4
+
+CHUNK = 16
+CHUNKS = B_TILES * GROUPS // CHUNK
+UNIT = 8
+BANK_GROUPS = 2
+X_BUFS = 3
+
 ROUND = 4
 ROUNDS = GROUPS // ROUND
-QUADRANTS = 4
-W2_LOAD_STEP = 4
+W_BUFS = 4
+TAPER = 2
 
 
 def tile_geometricmanifoldnetwork_pa_k_kernel(
@@ -34,7 +42,6 @@ def tile_geometricmanifoldnetwork_pa_k_kernel(
 ):
     nc = tc.nc
 
-    x_rows = x.rearrange("(t b) k -> b t k", b=P)
     w1_word_rows = W1_words.rearrange("g p n t -> g p (n t)").bitcast(I32)
     w1_scale_rows = W1_scales.bitcast(F32)
     w2_word_rows = W2_words.rearrange("g p n t -> g p (n t)").bitcast(I32)
@@ -42,11 +49,9 @@ def tile_geometricmanifoldnetwork_pa_k_kernel(
 
     with ExitStack() as ctx:
         const = ctx.enter_context(tc.tile_pool(name="const", bufs=1))
-        x_pool = ctx.enter_context(tc.tile_pool(name="x_pool", bufs=3))
-        sort_pool = ctx.enter_context(tc.tile_pool(name="sort_pool", bufs=2))
+        x_pool = ctx.enter_context(tc.tile_pool(name="x_pool", bufs=X_BUFS))
         group_pool = ctx.enter_context(tc.tile_pool(name="group_pool", bufs=2))
-        xq_pool = ctx.enter_context(tc.tile_pool(name="xq_pool", bufs=3))
-        w_pool = ctx.enter_context(tc.tile_pool(name="w_pool", bufs=6))
+        w_pool = ctx.enter_context(tc.tile_pool(name="w_pool", bufs=W_BUFS))
         tail = ctx.enter_context(tc.tile_pool(name="tail", bufs=1))
         acc_pool = ctx.enter_context(tc.psum_pool(name="acc_pool", bufs=1))
         work = ctx.enter_context(tc.psum_pool(name="work", bufs=4))
@@ -70,7 +75,6 @@ def tile_geometricmanifoldnetwork_pa_k_kernel(
         nc.vector.memset(w1_planes[:].bitcast(I32), 0)
         w2_planes = const.tile([P, M], U8, align_bytes=64)
         nc.vector.memset(w2_planes[:].bitcast(I32), 0)
-        w2_words = const.tile([P, F_HALVES, M], U32, align_bytes=64)
         for r in range(ROUNDS):
             for quadrant in range(QUADRANTS):
                 nc.gpsimd.dma_start(
@@ -109,107 +113,105 @@ def tile_geometricmanifoldnetwork_pa_k_kernel(
         )
         nc.scalar.copy(out=b2_spread[:], in_=b2_bank[:])
 
+        x_codes = const.tile([P, B_TILES * GROUPS * P], U32, align_bytes=64)
+        x_scales = const.tile([P, B_TILES * GROUPS * P], U8, align_bytes=64)
+        x_raw_of = {}
+
+        def load_x(chunk):
+            part, bt = divmod(chunk, B_TILES)
+            x_raw = x_pool.tile([P, CHUNK * K_PASS], BF16)
+            nc.sync.dma_start(
+                out=x_raw[:],
+                in_=x[bt * P : (bt + 1) * P, part * CHUNK * K_PASS : (part + 1) * CHUNK * K_PASS],
+            )
+            x_raw_of[chunk] = x_raw
+
+        def transpose_and_quantise(chunk, unit):
+            part, bt = divmod(chunk, B_TILES)
+            x_words = x_raw_of[chunk][:].bitcast(F32)
+            grouped = group_pool.tile([P, UNIT * P * PACK], BF16, align_bytes=64)
+            grouped_words = grouped[:].bitcast(F32).rearrange(
+                "q (n j b u) -> q n j b u", j=BANK_GROUPS, b=P, u=2
+            )
+            banks = UNIT // BANK_GROUPS
+            for n in range(banks):
+                xt = work.tile([P, BANK_GROUPS, 2, P], F32, tag="work")
+                for j in range(BANK_GROUPS):
+                    first_word = (unit * UNIT + n * BANK_GROUPS + j) * 2 * P
+                    for u in range(2):
+                        nc.tensor.transpose(
+                            xt[:, j, u, :],
+                            x_words[:, first_word + u : first_word + 2 * P : 2],
+                            ident_f32[:],
+                        )
+                if n < banks - 1:
+                    nc.scalar.copy(
+                        out=grouped_words[:, n], in_=xt[:].rearrange("q j u b -> q j b u")
+                    )
+                else:
+                    nc.vector.tensor_copy(
+                        out=grouped_words[:, n], in_=xt[:].rearrange("q j u b -> q j b u")
+                    )
+            first_group = bt * GROUPS + part * CHUNK + unit * UNIT
+            columns = slice(first_group * P, (first_group + UNIT) * P)
+            nc.vector.quantize_mx(
+                out=x_codes[:, columns].bitcast(FP8X4), scales=x_scales[:, columns], in_=grouped[:]
+            )
+
+        for chunk in range(X_BUFS):
+            load_x(chunk)
+        for chunk in range(CHUNKS):
+            for unit in range(CHUNK // UNIT):
+                transpose_and_quantise(chunk, unit)
+            if chunk + X_BUFS < CHUNKS:
+                load_x(chunk + X_BUFS)
+
         h_acc = {}
         for bt in range(B_TILES):
             for half in range(F_HALVES):
                 h_bank = acc_pool.tile([P, N_PASS], F32, name="h_acc_%d_%d" % (bt, half))
                 h_acc[(bt, half)] = h_bank
-
-        x_raw_of = {}
-        x_sorted_of = {}
-        x_codes_of = {}
-        x_scales_of = {}
         w_words_of = {}
 
-        def load_x(r):
-            x_raw = x_pool.tile([P, B_TILES, ROUND * K_PASS], BF16)
+        def load_w(r, first, count, columns):
             nc.sync.dma_start(
-                out=x_raw[:], in_=x_rows[:, :, r * ROUND * K_PASS : (r + 1) * ROUND * K_PASS]
+                out=w_words_of[r][:, first : first + count, columns].bitcast(I32),
+                in_=w1_word_rows[
+                    r * ROUND + first : r * ROUND + first + count, :, columns
+                ].rearrange("g p n -> p g n"),
             )
-            x_raw_of[r] = x_raw
 
-        def load_w(r):
+        def load_round(r):
             w_words = w_pool.tile([P, ROUND, F], U32, align_bytes=64)
-            step = 1 if r == ROUNDS - 1 else ROUND
-            for j in range(0, ROUND, step):
-                nc.sync.dma_start(
-                    out=w_words[:, j : j + step, :].bitcast(I32),
-                    in_=w1_word_rows[r * ROUND + j : r * ROUND + j + step].rearrange(
-                        "g p n -> p g n"
-                    ),
-                )
             w_words_of[r] = w_words
+            if r < ROUNDS - 1:
+                load_w(r, 0, ROUND, slice(0, F))
+                return
+            for j in range(ROUND - TAPER):
+                load_w(r, j, 1, slice(0, F))
+            for half in range(F_HALVES):
+                for j in range(ROUND - TAPER, ROUND):
+                    load_w(r, j, 1, slice(half * N_PASS, (half + 1) * N_PASS))
 
-        def sort_words(r):
-            x_sorted = sort_pool.tile([P, B_TILES * ROUND, 2, P], F32)
-            nc.vector.tensor_copy(
-                out=x_sorted[:],
-                in_=x_raw_of[r][:].bitcast(F32).rearrange("b t (g q u) -> b (t g) u q", q=P, u=2),
-            )
-            x_sorted_of[r] = x_sorted
-
-        def transpose_and_quantise(r):
-            x_sorted = x_sorted_of[r]
-            grouped = group_pool.tile([P, ROUND * B * PACK], BF16, align_bytes=64)
-            grouped_words = grouped[:].bitcast(F32).rearrange("q (g b u) -> q g b u", g=ROUND, u=2)
-            for j in range(ROUND):
-                xt = work.tile([P, 2, B], F32, tag="work")
-                for u in range(2):
-                    for bt in range(B_TILES):
-                        nc.tensor.transpose(
-                            xt[:, u, bt * P : (bt + 1) * P],
-                            x_sorted[:, bt * ROUND + j, u, :],
-                            ident_f32[:],
-                        )
-                nc.scalar.copy(out=grouped_words[:, j], in_=xt[:].rearrange("q u b -> q b u"))
-            x_codes = xq_pool.tile([P, ROUND * B], U32, align_bytes=64)
-            x_scales = xq_pool.tile([P, ROUND * B], U8, align_bytes=64)
-            nc.vector.quantize_mx(
-                out=x_codes[:].bitcast(FP8X4), scales=x_scales[:], in_=grouped[:]
-            )
-            x_codes_of[r] = x_codes
-            x_scales_of[r] = x_scales
-
-        def multiply(r):
-            for j in range(ROUND):
-                group = r * ROUND + j
-                for half in range(F_HALVES):
-                    for bt in range(B_TILES):
-                        rows = slice(j * B + bt * P, j * B + (bt + 1) * P)
-                        nc.tensor.matmul_mx(
-                            out=h_acc[(bt, half)][:],
-                            lhsT=x_codes_of[r][:, rows].bitcast(FP8X4),
-                            lhsT_scale=x_scales_of[r][:, rows],
-                            rhs=w_words_of[r][
-                                :, j, half * N_PASS : (half + 1) * N_PASS
-                            ].bitcast(FP8X4),
-                            rhs_scale=w1_planes[
-                                4 * j : P, r * F + half * N_PASS : r * F + (half + 1) * N_PASS
-                            ],
-                            start=(group == 0),
-                            stop=(group == GROUPS - 1),
-                        )
-
-        def load_w2():
-            nc.sync.dma_start(
-                out=w2_words[:].bitcast(I32), in_=w2_word_rows.rearrange("g p n -> p g n")
-            )
-
-        def if_round(stage, r):
-            if 0 <= r < ROUNDS:
-                stage(r)
-
-        for s in range(ROUNDS + 3):
-            if_round(load_w, s - 2)
-            if_round(load_x, s)
-            if s == W2_LOAD_STEP:
-                load_w2()
-            if_round(sort_words, s - 1)
-            if_round(transpose_and_quantise, s - 2)
-            if_round(multiply, s - 3)
+        def multiply(group, half):
+            r, j = divmod(group, ROUND)
+            for bt in range(B_TILES):
+                rows = slice((bt * GROUPS + group) * P, (bt * GROUPS + group + 1) * P)
+                nc.tensor.matmul_mx(
+                    out=h_acc[(bt, half)][:],
+                    lhsT=x_codes[:, rows].bitcast(FP8X4),
+                    lhsT_scale=x_scales[:, rows],
+                    rhs=w_words_of[r][:, j, half * N_PASS : (half + 1) * N_PASS].bitcast(FP8X4),
+                    rhs_scale=w1_planes[
+                        4 * j : P, r * F + half * N_PASS : r * F + (half + 1) * N_PASS
+                    ],
+                    start=(group == 0),
+                    stop=(group == GROUPS - 1),
+                )
 
         h_sorted = tail.tile([P, B_TILES, F_HALVES, PACK, P], BF16)
-        for half in range(F_HALVES):
+
+        def add_b1(half):
             for bt in range(B_TILES):
                 nc.vector.tensor_tensor(
                     out=h_sorted[:, bt, half],
@@ -218,39 +220,47 @@ def tile_geometricmanifoldnetwork_pa_k_kernel(
                     op=ALU.add,
                 )
 
+        for r in range(W_BUFS):
+            load_round(r)
+        for group in range(GROUPS - TAPER):
+            for half in range(F_HALVES):
+                multiply(group, half)
+            r, j = divmod(group, ROUND)
+            if j == ROUND - 1 and r + W_BUFS < ROUNDS:
+                load_round(r + W_BUFS)
+        w2_words = const.tile([P, F_HALVES, M], U32, align_bytes=64)
+        nc.sync.dma_start(
+            out=w2_words[:].bitcast(I32), in_=w2_word_rows.rearrange("g p n -> p g n")
+        )
+        for half in range(F_HALVES):
+            for group in range(GROUPS - TAPER, GROUPS):
+                multiply(group, half)
+            add_b1(half)
+
         h_grouped = tail.tile([P, F_HALVES, B, PACK], BF16, align_bytes=64)
         h_codes = tail.tile([P, F_HALVES * B], U32, align_bytes=64)
         h_scales = tail.tile([P, F_HALVES * B], U8, align_bytes=64)
-        ht_of = {}
 
-        def transpose_h(half):
+        for half in range(F_HALVES):
             for bt in range(B_TILES):
                 ht = work.tile([P, PACK, P], BF16, tag="work")
                 for t in range(PACK):
                     nc.tensor.transpose(ht[:, t, :], h_sorted[:, bt, half, t, :], ident_bf16[:])
-                ht_of[(bt, half)] = ht
-
-        def relu_and_quantise_h(half):
-            nc.scalar.activation(
-                out=h_grouped[:, half, 0:P, :],
-                in_=ht_of[(0, half)][:].rearrange("q t b -> q b t"),
-                func=ACT.Relu,
-            )
-            nc.vector.tensor_scalar_max(
-                out=h_grouped[:, half, P:B, :],
-                in0=ht_of[(1, half)][:].rearrange("q t b -> q b t"),
-                scalar1=0.0,
-            )
+                relu_out = h_grouped[:, half, bt * P : (bt + 1) * P, :]
+                if (half, bt) != (F_HALVES - 1, B_TILES - 1):
+                    nc.scalar.activation(
+                        out=relu_out, in_=ht[:].rearrange("q t b -> q b t"), func=ACT.Relu
+                    )
+                else:
+                    nc.vector.tensor_scalar_max(
+                        out=relu_out, in0=ht[:].rearrange("q t b -> q b t"), scalar1=0.0
+                    )
+        for half in range(F_HALVES):
             nc.vector.quantize_mx(
                 out=h_codes[:, half * B : (half + 1) * B].bitcast(FP8X4),
                 scales=h_scales[:, half * B : (half + 1) * B],
                 in_=h_grouped[:, half].rearrange("q b t -> q (b t)"),
             )
-
-        transpose_h(0)
-        transpose_h(1)
-        relu_and_quantise_h(0)
-        relu_and_quantise_h(1)
 
         v_acc = {}
         for bt in range(B_TILES):
@@ -275,7 +285,7 @@ def tile_geometricmanifoldnetwork_pa_k_kernel(
         clamped = tail.tile([P, B_TILES], F32)
         norm = tail.tile([P, B_TILES], F32)
         inv_norm = tail.tile([P, B_TILES], F32)
-        unit = tail.tile([P, B_TILES, M], F32)
+        unit_rows = tail.tile([P, B_TILES, M], F32)
         for bt in range(B_TILES):
             nc.vector.tensor_tensor(out=v[:, bt], in0=v_acc[bt][:], in1=b2_spread[:], op=ALU.add)
             nc.scalar.activation(
@@ -287,8 +297,9 @@ def tile_geometricmanifoldnetwork_pa_k_kernel(
         nc.vector.tensor_scalar_max(out=clamped[:], in0=sum_squares[:], scalar1=EPS * EPS)
         nc.scalar.activation(out=norm[:], in_=clamped[:], func=ACT.Sqrt)
         nc.vector.reciprocal(out=inv_norm[:], in_=norm[:])
+        nc.vector.tensor_scalar_mul(out=unit_rows[:, 0], in0=v[:, 0], scalar1=inv_norm[:, 0:1])
+        nc.scalar.activation(
+            out=unit_rows[:, 1], in_=v[:, 1], func=ACT.Copy, scale=inv_norm[:, 1:2]
+        )
         for bt in range(B_TILES):
-            nc.vector.tensor_scalar_mul(
-                out=unit[:, bt], in0=v[:, bt], scalar1=inv_norm[:, bt : bt + 1]
-            )
-            nc.sync.dma_start(out=out[bt * P : (bt + 1) * P, :], in_=unit[:, bt])
+            nc.sync.dma_start(out=out[bt * P : (bt + 1) * P, :], in_=unit_rows[:, bt])

@@ -25,11 +25,10 @@ F_HALVES = F // N_PASS
 GROUPS = IN // K_PASS
 QUADRANTS = 4
 
-CHUNK = 16
-CHUNKS = B_TILES * GROUPS // CHUNK
 UNIT = 8
+UNITS = B_TILES * GROUPS // UNIT
 BANK_GROUPS = 2
-X_BUFS = 3
+X_BUFS = 4
 
 ROUND = 4
 ROUNDS = GROUPS // ROUND
@@ -72,8 +71,9 @@ def tile_geometricmanifoldnetwork_pa_k_kernel(
         nc.vector.memset(ones[:], 1.0)
 
         w1_planes = const.tile([P, ROUNDS * F], U8, align_bytes=64)
-        nc.vector.memset(w1_planes[:].bitcast(I32), 0)
         w2_planes = const.tile([P, M], U8, align_bytes=64)
+        for r in range(ROUNDS):
+            nc.vector.memset(w1_planes[:, r * F : (r + 1) * F].bitcast(I32), 0)
         nc.vector.memset(w2_planes[:].bitcast(I32), 0)
         for r in range(ROUNDS):
             for quadrant in range(QUADRANTS):
@@ -95,40 +95,42 @@ def tile_geometricmanifoldnetwork_pa_k_kernel(
         nc.scalar.dma_start(out=bias_rows[0:1, F : F + M], in_=b2.rearrange("(o f) -> o f", o=1))
         b1_sorted = const.tile([P, F_HALVES, PACK, P], F32)
         b2_spread = const.tile([P, M], F32)
-        for half in range(F_HALVES):
-            b1_bank = work.tile([P, N_PASS], F32, tag="work")
+
+        def spread_biases():
+            for half in range(F_HALVES):
+                b1_bank = work.tile([P, N_PASS], F32, tag="work")
+                nc.tensor.matmul(
+                    out=b1_bank[:],
+                    lhsT=ones[:],
+                    rhs=bias_rows[:, half * N_PASS : (half + 1) * N_PASS],
+                    start=True,
+                    stop=True,
+                )
+                nc.scalar.copy(
+                    out=b1_sorted[:, half], in_=b1_bank[:].rearrange("b (q t) -> b t q", t=PACK)
+                )
+            b2_bank = work.tile([P, M], F32, tag="work")
             nc.tensor.matmul(
-                out=b1_bank[:],
-                lhsT=ones[:],
-                rhs=bias_rows[:, half * N_PASS : (half + 1) * N_PASS],
-                start=True,
-                stop=True,
+                out=b2_bank[:], lhsT=ones[:], rhs=bias_rows[:, F : F + M], start=True, stop=True
             )
-            nc.scalar.copy(
-                out=b1_sorted[:, half], in_=b1_bank[:].rearrange("b (q t) -> b t q", t=PACK)
-            )
-        b2_bank = work.tile([P, M], F32, tag="work")
-        nc.tensor.matmul(
-            out=b2_bank[:], lhsT=ones[:], rhs=bias_rows[:, F : F + M], start=True, stop=True
-        )
-        nc.scalar.copy(out=b2_spread[:], in_=b2_bank[:])
+            nc.scalar.copy(out=b2_spread[:], in_=b2_bank[:])
 
         x_codes = const.tile([P, B_TILES * GROUPS * P], U32, align_bytes=64)
         x_scales = const.tile([P, B_TILES * GROUPS * P], U8, align_bytes=64)
         x_raw_of = {}
 
-        def load_x(chunk):
-            part, bt = divmod(chunk, B_TILES)
-            x_raw = x_pool.tile([P, CHUNK * K_PASS], BF16)
+        def load_x(unit):
+            part, bt = divmod(unit, B_TILES)
+            x_raw = x_pool.tile([P, UNIT * K_PASS], BF16)
             nc.sync.dma_start(
                 out=x_raw[:],
-                in_=x[bt * P : (bt + 1) * P, part * CHUNK * K_PASS : (part + 1) * CHUNK * K_PASS],
+                in_=x[bt * P : (bt + 1) * P, part * UNIT * K_PASS : (part + 1) * UNIT * K_PASS],
             )
-            x_raw_of[chunk] = x_raw
+            x_raw_of[unit] = x_raw
 
-        def transpose_and_quantise(chunk, unit):
-            part, bt = divmod(chunk, B_TILES)
-            x_words = x_raw_of[chunk][:].bitcast(F32)
+        def transpose_and_quantise(unit):
+            part, bt = divmod(unit, B_TILES)
+            x_words = x_raw_of[unit][:].bitcast(F32)
             grouped = group_pool.tile([P, UNIT * P * PACK], BF16, align_bytes=64)
             grouped_words = grouped[:].bitcast(F32).rearrange(
                 "q (n j b u) -> q n j b u", j=BANK_GROUPS, b=P, u=2
@@ -137,7 +139,7 @@ def tile_geometricmanifoldnetwork_pa_k_kernel(
             for n in range(banks):
                 xt = work.tile([P, BANK_GROUPS, 2, P], F32, tag="work")
                 for j in range(BANK_GROUPS):
-                    first_word = (unit * UNIT + n * BANK_GROUPS + j) * 2 * P
+                    first_word = (n * BANK_GROUPS + j) * 2 * P
                     for u in range(2):
                         nc.tensor.transpose(
                             xt[:, j, u, :],
@@ -152,19 +154,11 @@ def tile_geometricmanifoldnetwork_pa_k_kernel(
                     nc.vector.tensor_copy(
                         out=grouped_words[:, n], in_=xt[:].rearrange("q j u b -> q j b u")
                     )
-            first_group = bt * GROUPS + part * CHUNK + unit * UNIT
+            first_group = bt * GROUPS + part * UNIT
             columns = slice(first_group * P, (first_group + UNIT) * P)
             nc.vector.quantize_mx(
                 out=x_codes[:, columns].bitcast(FP8X4), scales=x_scales[:, columns], in_=grouped[:]
             )
-
-        for chunk in range(X_BUFS):
-            load_x(chunk)
-        for chunk in range(CHUNKS):
-            for unit in range(CHUNK // UNIT):
-                transpose_and_quantise(chunk, unit)
-            if chunk + X_BUFS < CHUNKS:
-                load_x(chunk + X_BUFS)
 
         h_acc = {}
         for bt in range(B_TILES):
@@ -185,7 +179,8 @@ def tile_geometricmanifoldnetwork_pa_k_kernel(
             w_words = w_pool.tile([P, ROUND, F], U32, align_bytes=64)
             w_words_of[r] = w_words
             if r < ROUNDS - 1:
-                load_w(r, 0, ROUND, slice(0, F))
+                for j in range(0, ROUND, 2):
+                    load_w(r, j, 2, slice(0, F))
                 return
             for j in range(ROUND - TAPER):
                 load_w(r, j, 1, slice(0, F))
@@ -220,14 +215,31 @@ def tile_geometricmanifoldnetwork_pa_k_kernel(
                     op=ALU.add,
                 )
 
-        for r in range(W_BUFS):
-            load_round(r)
-        for group in range(GROUPS - TAPER):
-            for half in range(F_HALVES):
-                multiply(group, half)
-            r, j = divmod(group, ROUND)
-            if j == ROUND - 1 and r + W_BUFS < ROUNDS:
-                load_round(r + W_BUFS)
+        def multiply_round(r):
+            for j in range(ROUND):
+                if r * ROUND + j < GROUPS - TAPER:
+                    for half in range(F_HALVES):
+                        multiply(r * ROUND + j, half)
+
+        for unit in range(3):
+            load_x(unit)
+        load_round(0)
+        load_x(3)
+        load_round(1)
+        for unit in range(UNITS):
+            transpose_and_quantise(unit)
+            if unit + 4 < UNITS:
+                load_x(unit + 4)
+            if unit < 2:
+                load_round(unit + 2)
+            else:
+                multiply_round(unit - 2)
+                if unit + 2 < ROUNDS:
+                    load_round(unit + 2)
+            if unit == 3:
+                spread_biases()
+        multiply_round(ROUNDS - 2)
+        multiply_round(ROUNDS - 1)
         w2_words = const.tile([P, F_HALVES, M], U32, align_bytes=64)
         nc.sync.dma_start(
             out=w2_words[:].bitcast(I32), in_=w2_word_rows.rearrange("g p n -> p g n")

@@ -76,6 +76,12 @@ def tile_geometricmanifoldnetwork_pa_k_kernel(
             nc.vector.memset(w1_planes[:, r * F : (r + 1) * F].bitcast(I32), 0)
         nc.vector.memset(w2_planes[:].bitcast(I32), 0)
         for r in range(ROUNDS):
+            if r == ROUNDS // 2:
+                for quadrant in range(QUADRANTS):
+                    nc.gpsimd.dma_start(
+                        out=w2_planes[32 * quadrant : 32 * quadrant + 4 * F_HALVES, :].bitcast(F32),
+                        in_=w2_scale_rows[:, 4 * quadrant : 4 * quadrant + 4, :],
+                    )
             for quadrant in range(QUADRANTS):
                 nc.gpsimd.dma_start(
                     out=w1_planes[
@@ -85,11 +91,6 @@ def tile_geometricmanifoldnetwork_pa_k_kernel(
                         r * ROUND : (r + 1) * ROUND, 4 * quadrant : 4 * quadrant + 4, :
                     ],
                 )
-        for quadrant in range(QUADRANTS):
-            nc.gpsimd.dma_start(
-                out=w2_planes[32 * quadrant : 32 * quadrant + 4 * F_HALVES, :].bitcast(F32),
-                in_=w2_scale_rows[:, 4 * quadrant : 4 * quadrant + 4, :],
-            )
 
         nc.scalar.dma_start(out=bias_rows[0:1, 0:F], in_=b1.rearrange("(o f) -> o f", o=1))
         nc.scalar.dma_start(out=bias_rows[0:1, F : F + M], in_=b2.rearrange("(o f) -> o f", o=1))
@@ -178,15 +179,18 @@ def tile_geometricmanifoldnetwork_pa_k_kernel(
         def load_round(r):
             w_words = w_pool.tile([P, ROUND, F], U32, align_bytes=64)
             w_words_of[r] = w_words
-            if r < ROUNDS - 1:
+            if r < ROUNDS - TAPER:
                 for j in range(0, ROUND, 2):
                     load_w(r, j, 2, slice(0, F))
-                return
-            for j in range(ROUND - TAPER):
-                load_w(r, j, 1, slice(0, F))
-            for half in range(F_HALVES):
-                for j in range(ROUND - TAPER, ROUND):
-                    load_w(r, j, 1, slice(half * N_PASS, (half + 1) * N_PASS))
+
+        def load_taper(half):
+            columns = slice(half * N_PASS, (half + 1) * N_PASS)
+            for r in range(ROUNDS - TAPER, ROUNDS):
+                if half == F_HALVES - 1 and r == ROUNDS - 1:
+                    for j in range(0, ROUND, 2):
+                        load_w(r, j, 2, columns)
+                else:
+                    load_w(r, 0, ROUND, columns)
 
         def multiply(group, half):
             r, j = divmod(group, ROUND)
@@ -204,7 +208,17 @@ def tile_geometricmanifoldnetwork_pa_k_kernel(
                     stop=(group == GROUPS - 1),
                 )
 
+        def multiply_round(r, halves):
+            for j in range(ROUND):
+                for half in halves:
+                    multiply(r * ROUND + j, half)
+
         h_sorted = tail.tile([P, B_TILES, F_HALVES, PACK, P], BF16)
+        h_grouped = tail.tile([P, F_HALVES, B_TILES, P * PACK], BF16, align_bytes=64)
+        h_codes = tail.tile([P, F_HALVES * B], U32, align_bytes=64)
+        h_scales = tail.tile([P, F_HALVES * B], U8, align_bytes=64)
+        w2_words = const.tile([P, F_HALVES, M], U32, align_bytes=64)
+        v_acc = {}
 
         def add_b1(half):
             for bt in range(B_TILES):
@@ -215,12 +229,43 @@ def tile_geometricmanifoldnetwork_pa_k_kernel(
                     op=ALU.add,
                 )
 
-        def multiply_round(r):
-            for j in range(ROUND):
-                if r * ROUND + j < GROUPS - TAPER:
-                    for half in range(F_HALVES):
-                        multiply(r * ROUND + j, half)
+        def transpose_h(half):
+            for bt in range(B_TILES):
+                ht = work.tile([P, PACK, P], BF16, tag="work")
+                for t in range(PACK):
+                    nc.tensor.transpose(ht[:, t, :], h_sorted[:, bt, half, t, :], ident_bf16[:])
+                nc.scalar.activation(
+                    out=h_grouped[:, half, bt].rearrange("q (b t) -> q b t", t=PACK),
+                    in_=ht[:].rearrange("q t b -> q b t"),
+                    func=ACT.Relu,
+                )
 
+        def quantise_h(half):
+            for bt in range(B_TILES):
+                columns = slice((half * B_TILES + bt) * P, (half * B_TILES + bt + 1) * P)
+                nc.vector.quantize_mx(
+                    out=h_codes[:, columns].bitcast(FP8X4),
+                    scales=h_scales[:, columns],
+                    in_=h_grouped[:, half, bt],
+                )
+
+        def multiply_h(half):
+            for bt in range(B_TILES):
+                if half == 0:
+                    v_bank = work.tile([P, M], F32, tag="work")
+                    v_acc[bt] = v_bank
+                columns = slice((half * B_TILES + bt) * P, (half * B_TILES + bt + 1) * P)
+                nc.tensor.matmul_mx(
+                    out=v_acc[bt][:],
+                    lhsT=h_codes[:, columns].bitcast(FP8X4),
+                    lhsT_scale=h_scales[:, columns],
+                    rhs=w2_words[:, half, :].bitcast(FP8X4),
+                    rhs_scale=w2_planes[4 * half : P, :],
+                    start=(half == 0),
+                    stop=(half == F_HALVES - 1),
+                )
+
+        both = range(F_HALVES)
         for unit in range(3):
             load_x(unit)
         load_round(0)
@@ -233,63 +278,32 @@ def tile_geometricmanifoldnetwork_pa_k_kernel(
             if unit < 2:
                 load_round(unit + 2)
             else:
-                multiply_round(unit - 2)
+                multiply_round(unit - 2, both)
                 if unit + 2 < ROUNDS:
                     load_round(unit + 2)
             if unit == 3:
                 spread_biases()
-        multiply_round(ROUNDS - 2)
-        multiply_round(ROUNDS - 1)
-        w2_words = const.tile([P, F_HALVES, M], U32, align_bytes=64)
+        load_taper(0)
         nc.sync.dma_start(
             out=w2_words[:].bitcast(I32), in_=w2_word_rows.rearrange("g p n -> p g n")
         )
-        for half in range(F_HALVES):
-            for group in range(GROUPS - TAPER, GROUPS):
-                multiply(group, half)
-            add_b1(half)
+        load_taper(1)
 
-        h_grouped = tail.tile([P, F_HALVES, B, PACK], BF16, align_bytes=64)
-        h_codes = tail.tile([P, F_HALVES * B], U32, align_bytes=64)
-        h_scales = tail.tile([P, F_HALVES * B], U8, align_bytes=64)
-
-        for half in range(F_HALVES):
-            for bt in range(B_TILES):
-                ht = work.tile([P, PACK, P], BF16, tag="work")
-                for t in range(PACK):
-                    nc.tensor.transpose(ht[:, t, :], h_sorted[:, bt, half, t, :], ident_bf16[:])
-                relu_out = h_grouped[:, half, bt * P : (bt + 1) * P, :]
-                if (half, bt) != (F_HALVES - 1, B_TILES - 1):
-                    nc.scalar.activation(
-                        out=relu_out, in_=ht[:].rearrange("q t b -> q b t"), func=ACT.Relu
-                    )
-                else:
-                    nc.vector.tensor_scalar_max(
-                        out=relu_out, in0=ht[:].rearrange("q t b -> q b t"), scalar1=0.0
-                    )
-        for half in range(F_HALVES):
-            nc.vector.quantize_mx(
-                out=h_codes[:, half * B : (half + 1) * B].bitcast(FP8X4),
-                scales=h_scales[:, half * B : (half + 1) * B],
-                in_=h_grouped[:, half].rearrange("q b t -> q (b t)"),
-            )
-
-        v_acc = {}
-        for bt in range(B_TILES):
-            v_bank = work.tile([P, M], F32, tag="work")
-            v_acc[bt] = v_bank
-        for half in range(F_HALVES):
-            for bt in range(B_TILES):
-                rows = slice(half * B + bt * P, half * B + (bt + 1) * P)
-                nc.tensor.matmul_mx(
-                    out=v_acc[bt][:],
-                    lhsT=h_codes[:, rows].bitcast(FP8X4),
-                    lhsT_scale=h_scales[:, rows],
-                    rhs=w2_words[:, half, :].bitcast(FP8X4),
-                    rhs_scale=w2_planes[4 * half : P, :],
-                    start=(half == 0),
-                    stop=(half == F_HALVES - 1),
-                )
+        for r in range(ROUNDS - TAPER, ROUNDS):
+            multiply_round(r, [0])
+        add_b1(0)
+        multiply_round(ROUNDS - 2, [1])
+        transpose_h(0)
+        quantise_h(0)
+        for group in range(GROUPS - ROUND, GROUPS - 2):
+            multiply(group, 1)
+        multiply_h(0)
+        for group in range(GROUPS - 2, GROUPS):
+            multiply(group, 1)
+        add_b1(1)
+        transpose_h(1)
+        quantise_h(1)
+        multiply_h(1)
 
         v = tail.tile([P, B_TILES, M], F32)
         squares = tail.tile([P, B_TILES, M], F32)
@@ -306,12 +320,14 @@ def tile_geometricmanifoldnetwork_pa_k_kernel(
                 func=ACT.Square,
                 accum_out=sum_squares[:, bt : bt + 1],
             )
-        nc.vector.tensor_scalar_max(out=clamped[:], in0=sum_squares[:], scalar1=EPS * EPS)
-        nc.scalar.activation(out=norm[:], in_=clamped[:], func=ACT.Sqrt)
-        nc.vector.reciprocal(out=inv_norm[:], in_=norm[:])
-        nc.vector.tensor_scalar_mul(out=unit_rows[:, 0], in0=v[:, 0], scalar1=inv_norm[:, 0:1])
-        nc.scalar.activation(
-            out=unit_rows[:, 1], in_=v[:, 1], func=ACT.Copy, scale=inv_norm[:, 1:2]
-        )
         for bt in range(B_TILES):
+            column = slice(bt, bt + 1)
+            nc.vector.tensor_scalar_max(
+                out=clamped[:, column], in0=sum_squares[:, column], scalar1=EPS * EPS
+            )
+            nc.scalar.activation(out=norm[:, column], in_=clamped[:, column], func=ACT.Sqrt)
+            nc.vector.reciprocal(out=inv_norm[:, column], in_=norm[:, column])
+            nc.vector.tensor_scalar_mul(
+                out=unit_rows[:, bt], in0=v[:, bt], scalar1=inv_norm[:, column]
+            )
             nc.sync.dma_start(out=out[bt * P : (bt + 1) * P, :], in_=unit_rows[:, bt])

@@ -32,6 +32,7 @@ X_BUFS = 4
 
 ROUND = 4
 ROUNDS = GROUPS // ROUND
+EARLY = 2
 W_BUFS = 4
 TAPER = 2
 
@@ -65,32 +66,44 @@ def tile_geometricmanifoldnetwork_pa_k_kernel(
         ident_bf16 = const.tile([P, P], BF16)
         make_identity(nc, ident_bf16[:])
 
-        bias_rows = const.tile([P, F + M], BF16)
-        nc.vector.memset(bias_rows[:], 0.0)
-        ones = const.tile([P, P], BF16)
-        nc.vector.memset(ones[:], 1.0)
 
         w1_planes = const.tile([P, ROUNDS * F], U8, align_bytes=64)
         w2_planes = const.tile([P, M], U8, align_bytes=64)
         for r in range(ROUNDS):
             nc.vector.memset(w1_planes[:, r * F : (r + 1) * F].bitcast(I32), 0)
         nc.vector.memset(w2_planes[:].bitcast(I32), 0)
-        for r in range(ROUNDS):
-            if r == ROUNDS // 2:
-                for quadrant in range(QUADRANTS):
-                    nc.gpsimd.dma_start(
-                        out=w2_planes[32 * quadrant : 32 * quadrant + 4 * F_HALVES, :].bitcast(F32),
-                        in_=w2_scale_rows[:, 4 * quadrant : 4 * quadrant + 4, :],
-                    )
+
+        def load_early_scales(r):
             for quadrant in range(QUADRANTS):
-                nc.gpsimd.dma_start(
+                nc.sync.dma_start(
                     out=w1_planes[
                         32 * quadrant : 32 * quadrant + 4 * ROUND, r * F : (r + 1) * F
-                    ].bitcast(F32),
-                    in_=w1_scale_rows[
+                    ].bitcast(I32),
+                    in_=W1_scales[
                         r * ROUND : (r + 1) * ROUND, 4 * quadrant : 4 * quadrant + 4, :
-                    ],
+                    ].bitcast(I32),
                 )
+
+        by_plane = w1_scale_rows.rearrange("(r j) q n -> j q r n", j=ROUND)
+        for j in range(ROUND):
+            for quadrant in range(QUADRANTS):
+                first = 32 * quadrant + 4 * j
+                nc.gpsimd.dma_start(
+                    out=w1_planes[first : first + 4, EARLY * F :]
+                    .bitcast(F32)
+                    .rearrange("p (r n) -> p r n", r=ROUNDS - EARLY),
+                    in_=by_plane[j, 4 * quadrant : 4 * quadrant + 4, EARLY:, :],
+                )
+        for quadrant in range(QUADRANTS):
+            nc.gpsimd.dma_start(
+                out=w2_planes[32 * quadrant : 32 * quadrant + 4 * F_HALVES, :].bitcast(F32),
+                in_=w2_scale_rows[:, 4 * quadrant : 4 * quadrant + 4, :],
+            )
+
+        bias_rows = const.tile([P, F + M], BF16)
+        nc.vector.memset(bias_rows[:], 0.0)
+        ones = const.tile([P, P], BF16)
+        nc.vector.memset(ones[:], 1.0)
 
         nc.scalar.dma_start(out=bias_rows[0:1, 0:F], in_=b1.rearrange("(o f) -> o f", o=1))
         nc.scalar.dma_start(out=bias_rows[0:1, F : F + M], in_=b2.rearrange("(o f) -> o f", o=1))
@@ -266,8 +279,11 @@ def tile_geometricmanifoldnetwork_pa_k_kernel(
                 )
 
         both = range(F_HALVES)
-        for unit in range(3):
-            load_x(unit)
+        load_x(0)
+        load_early_scales(0)
+        load_x(1)
+        load_x(2)
+        load_early_scales(1)
         load_round(0)
         load_x(3)
         load_round(1)

@@ -32,7 +32,7 @@ X_BUFS = 4
 
 ROUND = 4
 ROUNDS = GROUPS // ROUND
-EARLY = 2
+EARLY = 4
 W_BUFS = 4
 TAPER = 2
 
@@ -84,15 +84,15 @@ def tile_geometricmanifoldnetwork_pa_k_kernel(
                     ].bitcast(I32),
                 )
 
-        by_plane = w1_scale_rows.rearrange("(r j) q n -> j q r n", j=ROUND)
-        for j in range(ROUND):
+        for r in range(EARLY, ROUNDS):
             for quadrant in range(QUADRANTS):
-                first = 32 * quadrant + 4 * j
                 nc.gpsimd.dma_start(
-                    out=w1_planes[first : first + 4, EARLY * F :]
-                    .bitcast(F32)
-                    .rearrange("p (r n) -> p r n", r=ROUNDS - EARLY),
-                    in_=by_plane[j, 4 * quadrant : 4 * quadrant + 4, EARLY:, :],
+                    out=w1_planes[
+                        32 * quadrant : 32 * quadrant + 4 * ROUND, r * F : (r + 1) * F
+                    ].bitcast(F32),
+                    in_=w1_scale_rows[
+                        r * ROUND : (r + 1) * ROUND, 4 * quadrant : 4 * quadrant + 4, :
+                    ],
                 )
         for quadrant in range(QUADRANTS):
             nc.gpsimd.dma_start(
@@ -286,12 +286,15 @@ def tile_geometricmanifoldnetwork_pa_k_kernel(
         load_early_scales(1)
         load_round(0)
         load_x(3)
+        load_early_scales(2)
         load_round(1)
         for unit in range(UNITS):
             transpose_and_quantise(unit)
             if unit + 4 < UNITS:
                 load_x(unit + 4)
             if unit < 2:
+                if unit == 0:
+                    load_early_scales(3)
                 load_round(unit + 2)
             else:
                 multiply_round(unit - 2, both)

@@ -28,11 +28,12 @@ QUADRANTS = 4
 UNIT = 8
 UNITS = B_TILES * GROUPS // UNIT
 BANK_GROUPS = 2
-X_BUFS = 4
+X_BUFS = 3
+SORT_FROM = 2
 
 ROUND = 4
 ROUNDS = GROUPS // ROUND
-EARLY = 4
+PARTS = GROUPS // UNIT
 W_BUFS = 4
 TAPER = 2
 
@@ -43,13 +44,13 @@ def tile_geometricmanifoldnetwork_pa_k_kernel(
     nc = tc.nc
 
     w1_word_rows = W1_words.rearrange("g p n t -> g p (n t)").bitcast(I32)
-    w1_scale_rows = W1_scales.bitcast(F32)
     w2_word_rows = W2_words.rearrange("g p n t -> g p (n t)").bitcast(I32)
     w2_scale_rows = W2_scales.bitcast(F32)
 
     with ExitStack() as ctx:
         const = ctx.enter_context(tc.tile_pool(name="const", bufs=1))
         x_pool = ctx.enter_context(tc.tile_pool(name="x_pool", bufs=X_BUFS))
+        sort_pool = ctx.enter_context(tc.tile_pool(name="sort_pool", bufs=2))
         group_pool = ctx.enter_context(tc.tile_pool(name="group_pool", bufs=2))
         w_pool = ctx.enter_context(tc.tile_pool(name="w_pool", bufs=W_BUFS))
         tail = ctx.enter_context(tc.tile_pool(name="tail", bufs=1))
@@ -59,7 +60,7 @@ def tile_geometricmanifoldnetwork_pa_k_kernel(
 
         warm = const.tile([P, 1], F32)
         nc.vector.memset(warm[:], 1.0)
-        nc.scalar.activation(out=warm[:], in_=warm[:], func=ACT.Sqrt)
+        nc.scalar.activation(out=warm[:], in_=warm[:], func=ACT.Abs_reciprocal_sqrt)
 
         ident_f32 = const.tile([P, P], F32)
         make_identity(nc, ident_f32[:])
@@ -67,48 +68,44 @@ def tile_geometricmanifoldnetwork_pa_k_kernel(
         make_identity(nc, ident_bf16[:])
 
 
-        w1_planes = const.tile([P, ROUNDS * F], U8, align_bytes=64)
+        w1_planes = []
+        for q in range(PARTS):
+            planes = const.tile([P, UNIT * F], U8, align_bytes=64, name="w1_planes_%d" % q)
+            w1_planes.append(planes)
         w2_planes = const.tile([P, M], U8, align_bytes=64)
-        for r in range(ROUNDS):
-            nc.vector.memset(w1_planes[:, r * F : (r + 1) * F].bitcast(I32), 0)
+
+        def zero_planes(q):
+            nc.vector.memset(w1_planes[q][:].bitcast(I32), 0)
+
+        def load_scales(q):
+            for quadrant in range(QUADRANTS):
+                live = w1_planes[q][32 * quadrant + 4 * q : 32 * quadrant + 4 * q + 4, :]
+                rows = W1_scales[q * UNIT : (q + 1) * UNIT, 4 * quadrant : 4 * quadrant + 4, :]
+                if q == 0:
+                    nc.sync.dma_start(
+                        out=live.bitcast(I32).rearrange("i (g n) -> i g n", g=UNIT),
+                        in_=rows.bitcast(I32).rearrange("g i n -> i g n"),
+                    )
+                else:
+                    nc.gpsimd.dma_start(
+                        out=live.bitcast(F32).rearrange("i (g n) -> i g n", g=UNIT),
+                        in_=rows.bitcast(F32).rearrange("g i n -> i g n"),
+                    )
+
+        zero_planes(0)
         nc.vector.memset(w2_planes[:].bitcast(I32), 0)
-
-        def load_early_scales(r):
-            for quadrant in range(QUADRANTS):
-                nc.sync.dma_start(
-                    out=w1_planes[
-                        32 * quadrant : 32 * quadrant + 4 * ROUND, r * F : (r + 1) * F
-                    ].bitcast(I32),
-                    in_=W1_scales[
-                        r * ROUND : (r + 1) * ROUND, 4 * quadrant : 4 * quadrant + 4, :
-                    ].bitcast(I32),
-                )
-
-        for r in range(EARLY, ROUNDS):
-            for quadrant in range(QUADRANTS):
-                nc.gpsimd.dma_start(
-                    out=w1_planes[
-                        32 * quadrant : 32 * quadrant + 4 * ROUND, r * F : (r + 1) * F
-                    ].bitcast(F32),
-                    in_=w1_scale_rows[
-                        r * ROUND : (r + 1) * ROUND, 4 * quadrant : 4 * quadrant + 4, :
-                    ],
-                )
-        for quadrant in range(QUADRANTS):
-            nc.gpsimd.dma_start(
-                out=w2_planes[32 * quadrant : 32 * quadrant + 4 * F_HALVES, :].bitcast(F32),
-                in_=w2_scale_rows[:, 4 * quadrant : 4 * quadrant + 4, :],
-            )
+        zero_planes(1)
+        load_scales(1)
 
         bias_rows = const.tile([P, F + M], BF16)
         nc.vector.memset(bias_rows[:], 0.0)
         ones = const.tile([P, P], BF16)
         nc.vector.memset(ones[:], 1.0)
 
-        nc.scalar.dma_start(out=bias_rows[0:1, 0:F], in_=b1.rearrange("(o f) -> o f", o=1))
-        nc.scalar.dma_start(out=bias_rows[0:1, F : F + M], in_=b2.rearrange("(o f) -> o f", o=1))
-        b1_sorted = const.tile([P, F_HALVES, PACK, P], F32)
-        b2_spread = const.tile([P, M], F32)
+        nc.gpsimd.dma_start(out=bias_rows[0:1, 0:F], in_=b1.rearrange("(o f) -> o f", o=1))
+        nc.gpsimd.dma_start(out=bias_rows[0:1, F : F + M], in_=b2.rearrange("(o f) -> o f", o=1))
+        b1_sorted = const.tile([P, F_HALVES, PACK, P], BF16)
+        b2_spread = const.tile([P, M], BF16)
 
         def spread_biases():
             for half in range(F_HALVES):
@@ -142,6 +139,16 @@ def tile_geometricmanifoldnetwork_pa_k_kernel(
             )
             x_raw_of[unit] = x_raw
 
+        sorted_of = {}
+
+        def sort_words(unit):
+            sorted_words = sort_pool.tile([P, UNIT * 2 * P], F32)
+            nc.vector.tensor_copy(
+                out=sorted_words[:].rearrange("b (g u q) -> b g u q", u=2, q=P),
+                in_=x_raw_of[unit][:].bitcast(F32).rearrange("b (g q u) -> b g u q", u=2, q=P),
+            )
+            sorted_of[unit] = sorted_words
+
         def transpose_and_quantise(unit):
             part, bt = divmod(unit, B_TILES)
             x_words = x_raw_of[unit][:].bitcast(F32)
@@ -155,11 +162,11 @@ def tile_geometricmanifoldnetwork_pa_k_kernel(
                 for j in range(BANK_GROUPS):
                     first_word = (n * BANK_GROUPS + j) * 2 * P
                     for u in range(2):
-                        nc.tensor.transpose(
-                            xt[:, j, u, :],
-                            x_words[:, first_word + u : first_word + 2 * P : 2],
-                            ident_f32[:],
-                        )
+                        if unit >= SORT_FROM:
+                            words = sorted_of[unit][:, first_word + u * P : first_word + (u + 1) * P]
+                        else:
+                            words = x_words[:, first_word + u : first_word + 2 * P : 2]
+                        nc.tensor.transpose(xt[:, j, u, :], words, ident_f32[:])
                 if n < banks - 1:
                     nc.scalar.copy(
                         out=grouped_words[:, n], in_=xt[:].rearrange("q j u b -> q j b u")
@@ -189,11 +196,12 @@ def tile_geometricmanifoldnetwork_pa_k_kernel(
                 ].rearrange("g p n -> p g n"),
             )
 
-        def load_round(r):
-            w_words = w_pool.tile([P, ROUND, F], U32, align_bytes=64)
-            w_words_of[r] = w_words
+        def load_round(r, pairs=range(0, ROUND, 2)):
+            if r not in w_words_of:
+                w_words = w_pool.tile([P, ROUND, F], U32, align_bytes=64)
+                w_words_of[r] = w_words
             if r < ROUNDS - TAPER:
-                for j in range(0, ROUND, 2):
+                for j in pairs:
                     load_w(r, j, 2, slice(0, F))
 
         def load_taper(half):
@@ -205,26 +213,29 @@ def tile_geometricmanifoldnetwork_pa_k_kernel(
                 else:
                     load_w(r, 0, ROUND, columns)
 
-        def multiply(group, half):
+        def multiply(group, half, b_tiles=range(B_TILES)):
             r, j = divmod(group, ROUND)
-            for bt in range(B_TILES):
+            q, i = divmod(group, UNIT)
+            for bt in b_tiles:
                 rows = slice((bt * GROUPS + group) * P, (bt * GROUPS + group + 1) * P)
                 nc.tensor.matmul_mx(
                     out=h_acc[(bt, half)][:],
                     lhsT=x_codes[:, rows].bitcast(FP8X4),
                     lhsT_scale=x_scales[:, rows],
                     rhs=w_words_of[r][:, j, half * N_PASS : (half + 1) * N_PASS].bitcast(FP8X4),
-                    rhs_scale=w1_planes[
-                        4 * j : P, r * F + half * N_PASS : r * F + (half + 1) * N_PASS
+                    rhs_scale=w1_planes[q][
+                        4 * q : P, i * F + half * N_PASS : i * F + (half + 1) * N_PASS
                     ],
                     start=(group == 0),
                     stop=(group == GROUPS - 1),
                 )
 
-        def multiply_round(r, halves):
-            for j in range(ROUND):
-                for half in halves:
-                    multiply(r * ROUND + j, half)
+        def multiply_round(r, halves, pairs=range(0, ROUND, 2)):
+            for first in pairs:
+                for bt in range(B_TILES):
+                    for j in range(first, first + 2):
+                        for half in halves:
+                            multiply(r * ROUND + j, half, [bt])
 
         h_sorted = tail.tile([P, B_TILES, F_HALVES, PACK, P], BF16)
         h_grouped = tail.tile([P, F_HALVES, B_TILES, P * PACK], BF16, align_bytes=64)
@@ -280,28 +291,46 @@ def tile_geometricmanifoldnetwork_pa_k_kernel(
 
         both = range(F_HALVES)
         load_x(0)
-        load_early_scales(0)
         load_x(1)
-        load_x(2)
-        load_early_scales(1)
+        load_scales(0)
         load_round(0)
+        load_x(2)
+        load_round(1, [0])
+        transpose_and_quantise(0)
         load_x(3)
-        load_early_scales(2)
-        load_round(1)
-        for unit in range(UNITS):
-            transpose_and_quantise(unit)
-            if unit + 4 < UNITS:
-                load_x(unit + 4)
-            if unit < 2:
-                if unit == 0:
-                    load_early_scales(3)
-                load_round(unit + 2)
-            else:
-                multiply_round(unit - 2, both)
-                if unit + 2 < ROUNDS:
-                    load_round(unit + 2)
-            if unit == 3:
+        load_round(1, [2])
+        transpose_and_quantise(1)
+        zero_planes(2)
+        load_scales(2)
+        load_x(4)
+        load_round(2)
+        multiply_round(0, both)
+        sort_words(2)
+        transpose_and_quantise(2)
+        zero_planes(3)
+        load_scales(3)
+        for quadrant in range(QUADRANTS):
+            nc.gpsimd.dma_start(
+                out=w2_planes[32 * quadrant : 32 * quadrant + 4 * F_HALVES, :].bitcast(F32),
+                in_=w2_scale_rows[:, 4 * quadrant : 4 * quadrant + 4, :],
+            )
+        load_x(5)
+        load_round(3)
+        multiply_round(1, both)
+        sort_words(3)
+        sort_words(4)
+        transpose_and_quantise(3)
+        for r in range(2, ROUNDS - TAPER):
+            if r > 2:
+                sort_words(r + 2)
+            transpose_and_quantise(r + 2)
+            if r + 4 < UNITS:
+                load_x(r + 4)
+            load_round(r + 2)
+            multiply_round(r, both, [0])
+            if r == 3:
                 spread_biases()
+            multiply_round(r, both, [2])
         load_taper(0)
         nc.sync.dma_start(
             out=w2_words[:].bitcast(I32), in_=w2_word_rows.rearrange("g p n -> p g n")
@@ -317,8 +346,9 @@ def tile_geometricmanifoldnetwork_pa_k_kernel(
         for group in range(GROUPS - ROUND, GROUPS - 2):
             multiply(group, 1)
         multiply_h(0)
-        for group in range(GROUPS - 2, GROUPS):
-            multiply(group, 1)
+        for bt in range(B_TILES):
+            for group in range(GROUPS - 2, GROUPS):
+                multiply(group, 1, [bt])
         add_b1(1)
         transpose_h(1)
         quantise_h(1)
@@ -326,27 +356,49 @@ def tile_geometricmanifoldnetwork_pa_k_kernel(
 
         v = tail.tile([P, B_TILES, M], F32)
         squares = tail.tile([P, B_TILES, M], F32)
-        sum_squares = tail.tile([P, B_TILES], F32)
+        sums = tail.tile([P, B_TILES, 2], F32)
         clamped = tail.tile([P, B_TILES], F32)
-        norm = tail.tile([P, B_TILES], F32)
         inv_norm = tail.tile([P, B_TILES], F32)
         unit_rows = tail.tile([P, B_TILES, M], F32)
+        column_halves = [slice(0, M // 2), slice(M // 2, M)]
         for bt in range(B_TILES):
-            nc.vector.tensor_tensor(out=v[:, bt], in0=v_acc[bt][:], in1=b2_spread[:], op=ALU.add)
+            for c, columns in enumerate(column_halves):
+                nc.vector.tensor_tensor(
+                    out=v[:, bt, columns],
+                    in0=v_acc[bt][:, columns],
+                    in1=b2_spread[:, columns],
+                    op=ALU.add,
+                )
+                nc.scalar.activation(
+                    out=squares[:, bt, columns],
+                    in_=v[:, bt, columns],
+                    func=ACT.Square,
+                    accum_out=sums[:, bt, c : c + 1],
+                )
+        for bt in range(B_TILES):
+            nc.vector.tensor_scalar(
+                out=clamped[:, bt : bt + 1],
+                in0=sums[:, bt, 0:1],
+                scalar1=sums[:, bt, 1:2],
+                scalar2=EPS * EPS,
+                op0=ALU.add,
+                op1=ALU.max,
+            )
             nc.scalar.activation(
-                out=squares[:, bt],
-                in_=v[:, bt],
-                func=ACT.Square,
-                accum_out=sum_squares[:, bt : bt + 1],
+                out=inv_norm[:, bt : bt + 1],
+                in_=clamped[:, bt : bt + 1],
+                func=ACT.Abs_reciprocal_sqrt,
             )
         for bt in range(B_TILES):
-            column = slice(bt, bt + 1)
-            nc.vector.tensor_scalar_max(
-                out=clamped[:, column], in0=sum_squares[:, column], scalar1=EPS * EPS
-            )
-            nc.scalar.activation(out=norm[:, column], in_=clamped[:, column], func=ACT.Sqrt)
-            nc.vector.reciprocal(out=inv_norm[:, column], in_=norm[:, column])
             nc.vector.tensor_scalar_mul(
-                out=unit_rows[:, bt], in0=v[:, bt], scalar1=inv_norm[:, column]
+                out=unit_rows[:, bt, column_halves[0]],
+                in0=v[:, bt, column_halves[0]],
+                scalar1=inv_norm[:, bt : bt + 1],
+            )
+            nc.scalar.activation(
+                out=unit_rows[:, bt, column_halves[1]],
+                in_=v[:, bt, column_halves[1]],
+                func=ACT.Copy,
+                scale=inv_norm[:, bt : bt + 1],
             )
             nc.sync.dma_start(out=out[bt * P : (bt + 1) * P, :], in_=unit_rows[:, bt])

@@ -28,14 +28,14 @@ QUADRANTS = 4
 UNIT = 8
 UNITS = B_TILES * GROUPS // UNIT
 BANK_GROUPS = 2
-X_BUFS = 3
+X_BUFS = 4
 SORT_FROM = 2
 
 ROUND = 4
 ROUNDS = GROUPS // ROUND
-PARTS = GROUPS // UNIT
+EARLY = 2
 W_BUFS = 4
-TAPER = 2
+TAPER = 1
 
 
 def tile_geometricmanifoldnetwork_pa_k_kernel(
@@ -68,42 +68,42 @@ def tile_geometricmanifoldnetwork_pa_k_kernel(
         make_identity(nc, ident_bf16[:])
 
 
-        w1_planes = []
-        for q in range(PARTS):
-            planes = const.tile([P, UNIT * F], U8, align_bytes=64, name="w1_planes_%d" % q)
-            w1_planes.append(planes)
+        w1_planes = const.tile([P, ROUNDS * F], U8, align_bytes=64)
         w2_planes = const.tile([P, M], U8, align_bytes=64)
-
-        def zero_planes(q):
-            nc.vector.memset(w1_planes[q][:].bitcast(I32), 0)
-
-        def load_scales(q):
-            for quadrant in range(QUADRANTS):
-                live = w1_planes[q][32 * quadrant + 4 * q : 32 * quadrant + 4 * q + 4, :]
-                rows = W1_scales[q * UNIT : (q + 1) * UNIT, 4 * quadrant : 4 * quadrant + 4, :]
-                if q == 0:
-                    nc.sync.dma_start(
-                        out=live.bitcast(I32).rearrange("i (g n) -> i g n", g=UNIT),
-                        in_=rows.bitcast(I32).rearrange("g i n -> i g n"),
-                    )
-                else:
-                    nc.gpsimd.dma_start(
-                        out=live.bitcast(F32).rearrange("i (g n) -> i g n", g=UNIT),
-                        in_=rows.bitcast(F32).rearrange("g i n -> i g n"),
-                    )
-
-        zero_planes(0)
+        for r in range(ROUNDS):
+            nc.vector.memset(w1_planes[:, r * F : (r + 1) * F].bitcast(I32), 0)
         nc.vector.memset(w2_planes[:].bitcast(I32), 0)
-        zero_planes(1)
-        load_scales(1)
+
+        def load_scales(r):
+            for quadrant in range(QUADRANTS):
+                live = w1_planes[
+                    32 * quadrant : 32 * quadrant + 4 * ROUND, r * F : (r + 1) * F
+                ]
+                rows = W1_scales[r * ROUND : (r + 1) * ROUND, 4 * quadrant : 4 * quadrant + 4, :]
+                if r < EARLY:
+                    nc.sync.dma_start(out=live.bitcast(I32), in_=rows.bitcast(I32))
+                else:
+                    nc.gpsimd.dma_start(out=live.bitcast(F32), in_=rows.bitcast(F32))
+
+        for r in range(EARLY, EARLY + 2):
+            load_scales(r)
 
         bias_rows = const.tile([P, F + M], BF16)
         nc.vector.memset(bias_rows[:], 0.0)
         ones = const.tile([P, P], BF16)
         nc.vector.memset(ones[:], 1.0)
 
-        nc.gpsimd.dma_start(out=bias_rows[0:1, 0:F], in_=b1.rearrange("(o f) -> o f", o=1))
-        nc.gpsimd.dma_start(out=bias_rows[0:1, F : F + M], in_=b2.rearrange("(o f) -> o f", o=1))
+        for r in range(EARLY + 2, ROUNDS):
+            load_scales(r)
+        for quadrant in range(QUADRANTS):
+            nc.gpsimd.dma_start(
+                out=w2_planes[32 * quadrant : 32 * quadrant + 4 * F_HALVES, :].bitcast(F32),
+                in_=w2_scale_rows[:, 4 * quadrant : 4 * quadrant + 4, :],
+            )
+        def load_biases():
+            nc.sync.dma_start(out=bias_rows[0:1, 0:F], in_=b1.rearrange("(o f) -> o f", o=1))
+            nc.sync.dma_start(out=bias_rows[0:1, F : F + M], in_=b2.rearrange("(o f) -> o f", o=1))
+
         b1_sorted = const.tile([P, F_HALVES, PACK, P], BF16)
         b2_spread = const.tile([P, M], BF16)
 
@@ -130,14 +130,16 @@ def tile_geometricmanifoldnetwork_pa_k_kernel(
         x_scales = const.tile([P, B_TILES * GROUPS * P], U8, align_bytes=64)
         x_raw_of = {}
 
-        def load_x(unit):
+        def load_x(unit, first=0, count=UNIT):
             part, bt = divmod(unit, B_TILES)
-            x_raw = x_pool.tile([P, UNIT * K_PASS], BF16)
+            if unit not in x_raw_of:
+                x_raw = x_pool.tile([P, UNIT * K_PASS], BF16)
+                x_raw_of[unit] = x_raw
+            start = (part * UNIT + first) * K_PASS
             nc.sync.dma_start(
-                out=x_raw[:],
-                in_=x[bt * P : (bt + 1) * P, part * UNIT * K_PASS : (part + 1) * UNIT * K_PASS],
+                out=x_raw_of[unit][:, first * K_PASS : (first + count) * K_PASS],
+                in_=x[bt * P : (bt + 1) * P, start : start + count * K_PASS],
             )
-            x_raw_of[unit] = x_raw
 
         sorted_of = {}
 
@@ -149,15 +151,15 @@ def tile_geometricmanifoldnetwork_pa_k_kernel(
             )
             sorted_of[unit] = sorted_words
 
-        def transpose_and_quantise(unit):
+        def transpose_and_quantise(unit, first=0, count=UNIT):
             part, bt = divmod(unit, B_TILES)
             x_words = x_raw_of[unit][:].bitcast(F32)
             grouped = group_pool.tile([P, UNIT * P * PACK], BF16, align_bytes=64)
             grouped_words = grouped[:].bitcast(F32).rearrange(
                 "q (n j b u) -> q n j b u", j=BANK_GROUPS, b=P, u=2
             )
-            banks = UNIT // BANK_GROUPS
-            for n in range(banks):
+            banks = range(first // BANK_GROUPS, (first + count) // BANK_GROUPS)
+            for n in banks:
                 xt = work.tile([P, BANK_GROUPS, 2, P], F32, tag="work")
                 for j in range(BANK_GROUPS):
                     first_word = (n * BANK_GROUPS + j) * 2 * P
@@ -167,7 +169,7 @@ def tile_geometricmanifoldnetwork_pa_k_kernel(
                         else:
                             words = x_words[:, first_word + u : first_word + 2 * P : 2]
                         nc.tensor.transpose(xt[:, j, u, :], words, ident_f32[:])
-                if n < banks - 1:
+                if n < banks[-1]:
                     nc.scalar.copy(
                         out=grouped_words[:, n], in_=xt[:].rearrange("q j u b -> q j b u")
                     )
@@ -175,10 +177,12 @@ def tile_geometricmanifoldnetwork_pa_k_kernel(
                     nc.vector.tensor_copy(
                         out=grouped_words[:, n], in_=xt[:].rearrange("q j u b -> q j b u")
                     )
-            first_group = bt * GROUPS + part * UNIT
-            columns = slice(first_group * P, (first_group + UNIT) * P)
+            first_group = bt * GROUPS + part * UNIT + first
+            columns = slice(first_group * P, (first_group + count) * P)
             nc.vector.quantize_mx(
-                out=x_codes[:, columns].bitcast(FP8X4), scales=x_scales[:, columns], in_=grouped[:]
+                out=x_codes[:, columns].bitcast(FP8X4),
+                scales=x_scales[:, columns],
+                in_=grouped[:, first * P * PACK : (first + count) * P * PACK],
             )
 
         h_acc = {}
@@ -215,7 +219,6 @@ def tile_geometricmanifoldnetwork_pa_k_kernel(
 
         def multiply(group, half, b_tiles=range(B_TILES)):
             r, j = divmod(group, ROUND)
-            q, i = divmod(group, UNIT)
             for bt in b_tiles:
                 rows = slice((bt * GROUPS + group) * P, (bt * GROUPS + group + 1) * P)
                 nc.tensor.matmul_mx(
@@ -223,8 +226,8 @@ def tile_geometricmanifoldnetwork_pa_k_kernel(
                     lhsT=x_codes[:, rows].bitcast(FP8X4),
                     lhsT_scale=x_scales[:, rows],
                     rhs=w_words_of[r][:, j, half * N_PASS : (half + 1) * N_PASS].bitcast(FP8X4),
-                    rhs_scale=w1_planes[q][
-                        4 * q : P, i * F + half * N_PASS : i * F + (half + 1) * N_PASS
+                    rhs_scale=w1_planes[
+                        4 * j : P, r * F + half * N_PASS : r * F + (half + 1) * N_PASS
                     ],
                     start=(group == 0),
                     stop=(group == GROUPS - 1),
@@ -290,72 +293,68 @@ def tile_geometricmanifoldnetwork_pa_k_kernel(
                 )
 
         both = range(F_HALVES)
-        load_x(0)
-        load_x(1)
+        load_x(0, 0, ROUND)
+        load_x(1, 0, ROUND)
         load_scales(0)
         load_round(0)
-        load_x(2)
+        load_x(0, ROUND, ROUND)
+        load_x(1, ROUND, ROUND)
+        load_scales(1)
         load_round(1, [0])
-        transpose_and_quantise(0)
-        load_x(3)
+        load_x(2)
         load_round(1, [2])
-        transpose_and_quantise(1)
-        zero_planes(2)
-        load_scales(2)
+        transpose_and_quantise(0, 0, ROUND)
+        transpose_and_quantise(1, 0, ROUND)
+        multiply_round(0, both)
+        transpose_and_quantise(0, ROUND, ROUND)
+        load_x(3)
+        transpose_and_quantise(1, ROUND, ROUND)
         load_x(4)
         load_round(2)
-        multiply_round(0, both)
+        multiply_round(1, both, [0])
         sort_words(2)
         transpose_and_quantise(2)
-        zero_planes(3)
-        load_scales(3)
-        for quadrant in range(QUADRANTS):
-            nc.gpsimd.dma_start(
-                out=w2_planes[32 * quadrant : 32 * quadrant + 4 * F_HALVES, :].bitcast(F32),
-                in_=w2_scale_rows[:, 4 * quadrant : 4 * quadrant + 4, :],
-            )
         load_x(5)
         load_round(3)
-        multiply_round(1, both)
+        multiply_round(1, both, [2])
         sort_words(3)
         sort_words(4)
         transpose_and_quantise(3)
+        load_biases()
         for r in range(2, ROUNDS - TAPER):
-            if r > 2:
-                sort_words(r + 2)
-            transpose_and_quantise(r + 2)
+            if r + 2 < UNITS:
+                if r > 2:
+                    sort_words(r + 2)
+                transpose_and_quantise(r + 2)
             if r + 4 < UNITS:
                 load_x(r + 4)
-            load_round(r + 2)
+            if r + 2 < ROUNDS:
+                load_round(r + 2)
+            if r + 2 == ROUNDS - 1:
+                load_taper(0)
+                nc.sync.dma_start(
+                    out=w2_words[:].bitcast(I32), in_=w2_word_rows.rearrange("g p n -> p g n")
+                )
+                load_taper(1)
             multiply_round(r, both, [0])
             if r == 3:
                 spread_biases()
             multiply_round(r, both, [2])
-        load_taper(0)
-        nc.sync.dma_start(
-            out=w2_words[:].bitcast(I32), in_=w2_word_rows.rearrange("g p n -> p g n")
-        )
-        load_taper(1)
 
-        for r in range(ROUNDS - TAPER, ROUNDS):
-            multiply_round(r, [0])
+        last = ROUNDS - 1
+        multiply_round(last, [0])
         add_b1(0)
-        multiply_round(ROUNDS - 2, [1])
+        multiply_round(last, [1], [0])
         transpose_h(0)
         quantise_h(0)
-        for group in range(GROUPS - ROUND, GROUPS - 2):
-            multiply(group, 1)
-        multiply_h(0)
-        for bt in range(B_TILES):
-            for group in range(GROUPS - 2, GROUPS):
-                multiply(group, 1, [bt])
+        multiply_round(last, [1], [2])
         add_b1(1)
         transpose_h(1)
+        multiply_h(0)
         quantise_h(1)
         multiply_h(1)
 
         v = tail.tile([P, B_TILES, M], F32)
-        squares = tail.tile([P, B_TILES, M], F32)
         sums = tail.tile([P, B_TILES, 2], F32)
         clamped = tail.tile([P, B_TILES], F32)
         inv_norm = tail.tile([P, B_TILES], F32)
@@ -370,7 +369,7 @@ def tile_geometricmanifoldnetwork_pa_k_kernel(
                     op=ALU.add,
                 )
                 nc.scalar.activation(
-                    out=squares[:, bt, columns],
+                    out=unit_rows[:, bt, columns],
                     in_=v[:, bt, columns],
                     func=ACT.Square,
                     accum_out=sums[:, bt, c : c + 1],

from contextlib import ExitStack

import concourse.mybir as mybir
from concourse.masks import make_identity

BF16 = mybir.dt.bfloat16
F32 = mybir.dt.float32
I32 = mybir.dt.int32
U32 = mybir.dt.uint32
U8 = mybir.dt.uint8
FP8X4 = mybir.dt.float8_e4m3fn_x4
ALU = mybir.AluOpType
ACT = mybir.ActivationFunctionType

B, IN, F, M = 256, 16384, 1024, 512
EPS = 1e-12
FLOPS = 2 * B * IN * F + 2 * B * F * M

P = 128
PACK = 4
K_PASS = P * PACK
N_PASS = 512
B_TILES = B // P
F_HALVES = F // N_PASS
GROUPS = IN // K_PASS
QUADRANTS = 4

UNIT = 8
UNITS = B_TILES * GROUPS // UNIT
BANK_GROUPS = 2
X_BUFS = 4
SORT_FROM = 2

ROUND = 4
ROUNDS = GROUPS // ROUND
EARLY = 2
W_BUFS = 4
TAPER = 1


def tile_geometricmanifoldnetwork_pa_k_kernel(
    tc, x, W1_words, W1_scales, b1, W2_words, W2_scales, b2, out
):
    nc = tc.nc

    w1_word_rows = W1_words.rearrange("g p n t -> g p (n t)").bitcast(I32)
    w2_word_rows = W2_words.rearrange("g p n t -> g p (n t)").bitcast(I32)
    w2_scale_rows = W2_scales.bitcast(F32)

    with ExitStack() as ctx:
        const = ctx.enter_context(tc.tile_pool(name="const", bufs=1))
        x_pool = ctx.enter_context(tc.tile_pool(name="x_pool", bufs=X_BUFS))
        sort_pool = ctx.enter_context(tc.tile_pool(name="sort_pool", bufs=2))
        group_pool = ctx.enter_context(tc.tile_pool(name="group_pool", bufs=2))
        w_pool = ctx.enter_context(tc.tile_pool(name="w_pool", bufs=W_BUFS))
        tail = ctx.enter_context(tc.tile_pool(name="tail", bufs=1))
        acc_pool = ctx.enter_context(tc.psum_pool(name="acc_pool", bufs=1))
        work = ctx.enter_context(tc.psum_pool(name="work", bufs=4))
        ctx.enter_context(tc.manual_schedule())

        warm = const.tile([P, 1], F32)
        nc.vector.memset(warm[:], 1.0)
        nc.scalar.activation(out=warm[:], in_=warm[:], func=ACT.Abs_reciprocal_sqrt)

        ident_f32 = const.tile([P, P], F32)
        make_identity(nc, ident_f32[:])
        ident_bf16 = const.tile([P, P], BF16)
        make_identity(nc, ident_bf16[:])


        w1_planes = const.tile([P, ROUNDS * F], U8, align_bytes=64)
        w2_planes = const.tile([P, M], U8, align_bytes=64)
        for r in range(ROUNDS):
            nc.vector.memset(w1_planes[:, r * F : (r + 1) * F].bitcast(I32), 0)
        nc.vector.memset(w2_planes[:].bitcast(I32), 0)

        def load_scales(r):
            for quadrant in range(QUADRANTS):
                live = w1_planes[
                    32 * quadrant : 32 * quadrant + 4 * ROUND, r * F : (r + 1) * F
                ]
                rows = W1_scales[r * ROUND : (r + 1) * ROUND, 4 * quadrant : 4 * quadrant + 4, :]
                if r < EARLY:
                    nc.sync.dma_start(out=live.bitcast(I32), in_=rows.bitcast(I32))
                else:
                    nc.gpsimd.dma_start(out=live.bitcast(F32), in_=rows.bitcast(F32))

        for r in range(EARLY, EARLY + 2):
            load_scales(r)

        bias_rows = const.tile([P, F + M], BF16)
        nc.vector.memset(bias_rows[:], 0.0)
        ones = const.tile([P, P], BF16)
        nc.vector.memset(ones[:], 1.0)

        for r in range(EARLY + 2, ROUNDS):
            load_scales(r)
        for quadrant in range(QUADRANTS):
            nc.gpsimd.dma_start(
                out=w2_planes[32 * quadrant : 32 * quadrant + 4 * F_HALVES, :].bitcast(F32),
                in_=w2_scale_rows[:, 4 * quadrant : 4 * quadrant + 4, :],
            )
        def load_biases():
            nc.sync.dma_start(out=bias_rows[0:1, 0:F], in_=b1.rearrange("(o f) -> o f", o=1))
            nc.sync.dma_start(out=bias_rows[0:1, F : F + M], in_=b2.rearrange("(o f) -> o f", o=1))

        b1_sorted = const.tile([P, F_HALVES, PACK, P], BF16)
        b2_spread = const.tile([P, M], BF16)

        def spread_biases():
            for half in range(F_HALVES):
                b1_bank = work.tile([P, N_PASS], F32, tag="work")
                nc.tensor.matmul(
                    out=b1_bank[:],
                    lhsT=ones[:],
                    rhs=bias_rows[:, half * N_PASS : (half + 1) * N_PASS],
                    start=True,
                    stop=True,
                )
                nc.scalar.copy(
                    out=b1_sorted[:, half], in_=b1_bank[:].rearrange("b (q t) -> b t q", t=PACK)
                )
            b2_bank = work.tile([P, M], F32, tag="work")
            nc.tensor.matmul(
                out=b2_bank[:], lhsT=ones[:], rhs=bias_rows[:, F : F + M], start=True, stop=True
            )
            nc.scalar.copy(out=b2_spread[:], in_=b2_bank[:])

        x_codes = const.tile([P, B_TILES * GROUPS * P], U32, align_bytes=64)
        x_scales = const.tile([P, B_TILES * GROUPS * P], U8, align_bytes=64)
        x_raw_of = {}

        def load_x(unit, first=0, count=UNIT):
            part, bt = divmod(unit, B_TILES)
            if unit not in x_raw_of:
                x_raw = x_pool.tile([P, UNIT * K_PASS], BF16)
                x_raw_of[unit] = x_raw
            start = (part * UNIT + first) * K_PASS
            nc.sync.dma_start(
                out=x_raw_of[unit][:, first * K_PASS : (first + count) * K_PASS],
                in_=x[bt * P : (bt + 1) * P, start : start + count * K_PASS],
            )

        sorted_of = {}

        def sort_words(unit):
            sorted_words = sort_pool.tile([P, UNIT * 2 * P], F32)
            nc.vector.tensor_copy(
                out=sorted_words[:].rearrange("b (g u q) -> b g u q", u=2, q=P),
                in_=x_raw_of[unit][:].bitcast(F32).rearrange("b (g q u) -> b g u q", u=2, q=P),
            )
            sorted_of[unit] = sorted_words

        def transpose_and_quantise(unit, first=0, count=UNIT):
            part, bt = divmod(unit, B_TILES)
            x_words = x_raw_of[unit][:].bitcast(F32)
            grouped = group_pool.tile([P, UNIT * P * PACK], BF16, align_bytes=64)
            grouped_words = grouped[:].bitcast(F32).rearrange(
                "q (n j b u) -> q n j b u", j=BANK_GROUPS, b=P, u=2
            )
            banks = range(first // BANK_GROUPS, (first + count) // BANK_GROUPS)
            for n in banks:
                xt = work.tile([P, BANK_GROUPS, 2, P], F32, tag="work")
                for j in range(BANK_GROUPS):
                    first_word = (n * BANK_GROUPS + j) * 2 * P
                    for u in range(2):
                        if unit >= SORT_FROM:
                            words = sorted_of[unit][:, first_word + u * P : first_word + (u + 1) * P]
                        else:
                            words = x_words[:, first_word + u : first_word + 2 * P : 2]
                        nc.tensor.transpose(xt[:, j, u, :], words, ident_f32[:])
                if n < banks[-1]:
                    nc.scalar.copy(
                        out=grouped_words[:, n], in_=xt[:].rearrange("q j u b -> q j b u")
                    )
                else:
                    nc.vector.tensor_copy(
                        out=grouped_words[:, n], in_=xt[:].rearrange("q j u b -> q j b u")
                    )
            first_group = bt * GROUPS + part * UNIT + first
            columns = slice(first_group * P, (first_group + count) * P)
            nc.vector.quantize_mx(
                out=x_codes[:, columns].bitcast(FP8X4),
                scales=x_scales[:, columns],
                in_=grouped[:, first * P * PACK : (first + count) * P * PACK],
            )

        h_acc = {}
        for bt in range(B_TILES):
            for half in range(F_HALVES):
                h_bank = acc_pool.tile([P, N_PASS], F32, name="h_acc_%d_%d" % (bt, half))
                h_acc[(bt, half)] = h_bank
        w_words_of = {}

        def load_w(r, first, count, columns):
            nc.sync.dma_start(
                out=w_words_of[r][:, first : first + count, columns].bitcast(I32),
                in_=w1_word_rows[
                    r * ROUND + first : r * ROUND + first + count, :, columns
                ].rearrange("g p n -> p g n"),
            )

        def load_round(r, pairs=range(0, ROUND, 2)):
            if r not in w_words_of:
                w_words = w_pool.tile([P, ROUND, F], U32, align_bytes=64)
                w_words_of[r] = w_words
            if r < ROUNDS - TAPER:
                for j in pairs:
                    load_w(r, j, 2, slice(0, F))

        def load_taper(half):
            columns = slice(half * N_PASS, (half + 1) * N_PASS)
            for r in range(ROUNDS - TAPER, ROUNDS):
                if half == F_HALVES - 1 and r == ROUNDS - 1:
                    for j in range(0, ROUND, 2):
                        load_w(r, j, 2, columns)
                else:
                    load_w(r, 0, ROUND, columns)

        def multiply(group, half, b_tiles=range(B_TILES)):
            r, j = divmod(group, ROUND)
            for bt in b_tiles:
                rows = slice((bt * GROUPS + group) * P, (bt * GROUPS + group + 1) * P)
                nc.tensor.matmul_mx(
                    out=h_acc[(bt, half)][:],
                    lhsT=x_codes[:, rows].bitcast(FP8X4),
                    lhsT_scale=x_scales[:, rows],
                    rhs=w_words_of[r][:, j, half * N_PASS : (half + 1) * N_PASS].bitcast(FP8X4),
                    rhs_scale=w1_planes[
                        4 * j : P, r * F + half * N_PASS : r * F + (half + 1) * N_PASS
                    ],
                    start=(group == 0),
                    stop=(group == GROUPS - 1),
                )

        def multiply_round(r, halves, pairs=range(0, ROUND, 2)):
            for first in pairs:
                for bt in range(B_TILES):
                    for j in range(first, first + 2):
                        for half in halves:
                            multiply(r * ROUND + j, half, [bt])

        h_sorted = tail.tile([P, B_TILES, F_HALVES, PACK, P], BF16)
        h_grouped = tail.tile([P, F_HALVES, B_TILES, P * PACK], BF16, align_bytes=64)
        h_codes = tail.tile([P, F_HALVES * B], U32, align_bytes=64)
        h_scales = tail.tile([P, F_HALVES * B], U8, align_bytes=64)
        w2_words = const.tile([P, F_HALVES, M], U32, align_bytes=64)
        v_acc = {}

        def add_b1(half):
            for bt in range(B_TILES):
                nc.vector.tensor_tensor(
                    out=h_sorted[:, bt, half],
                    in0=h_acc[(bt, half)][:].rearrange("b (q t) -> b t q", t=PACK),
                    in1=b1_sorted[:, half],
                    op=ALU.add,
                )

        def transpose_h(half):
            for bt in range(B_TILES):
                ht = work.tile([P, PACK, P], BF16, tag="work")
                for t in range(PACK):
                    nc.tensor.transpose(ht[:, t, :], h_sorted[:, bt, half, t, :], ident_bf16[:])
                nc.scalar.activation(
                    out=h_grouped[:, half, bt].rearrange("q (b t) -> q b t", t=PACK),
                    in_=ht[:].rearrange("q t b -> q b t"),
                    func=ACT.Relu,
                )

        def quantise_h(half):
            for bt in range(B_TILES):
                columns = slice((half * B_TILES + bt) * P, (half * B_TILES + bt + 1) * P)
                nc.vector.quantize_mx(
                    out=h_codes[:, columns].bitcast(FP8X4),
                    scales=h_scales[:, columns],
                    in_=h_grouped[:, half, bt],
                )

        def multiply_h(half):
            for bt in range(B_TILES):
                if half == 0:
                    v_bank = work.tile([P, M], F32, tag="work")
                    v_acc[bt] = v_bank
                columns = slice((half * B_TILES + bt) * P, (half * B_TILES + bt + 1) * P)
                nc.tensor.matmul_mx(
                    out=v_acc[bt][:],
                    lhsT=h_codes[:, columns].bitcast(FP8X4),
                    lhsT_scale=h_scales[:, columns],
                    rhs=w2_words[:, half, :].bitcast(FP8X4),
                    rhs_scale=w2_planes[4 * half : P, :],
                    start=(half == 0),
                    stop=(half == F_HALVES - 1),
                )

        both = range(F_HALVES)
        load_x(0, 0, ROUND)
        load_x(1, 0, ROUND)
        load_scales(0)
        load_round(0)
        load_x(0, ROUND, ROUND)
        load_x(1, ROUND, ROUND)
        load_scales(1)
        load_round(1, [0])
        load_x(2)
        load_round(1, [2])
        transpose_and_quantise(0, 0, ROUND)
        transpose_and_quantise(1, 0, ROUND)
        multiply_round(0, both)
        transpose_and_quantise(0, ROUND, ROUND)
        load_x(3)
        transpose_and_quantise(1, ROUND, ROUND)
        load_x(4)
        load_round(2)
        multiply_round(1, both, [0])
        sort_words(2)
        transpose_and_quantise(2)
        load_x(5)
        load_round(3)
        multiply_round(1, both, [2])
        sort_words(3)
        sort_words(4)
        transpose_and_quantise(3)
        load_biases()
        for r in range(2, ROUNDS - TAPER):
            if r + 2 < UNITS:
                if r > 2:
                    sort_words(r + 2)
                transpose_and_quantise(r + 2)
            if r + 4 < UNITS:
                load_x(r + 4)
            if r + 2 < ROUNDS:
                load_round(r + 2)
            if r + 2 == ROUNDS - 1:
                load_taper(0)
                nc.sync.dma_start(
                    out=w2_words[:].bitcast(I32), in_=w2_word_rows.rearrange("g p n -> p g n")
                )
                load_taper(1)
            multiply_round(r, both, [0])
            if r == 3:
                spread_biases()
            multiply_round(r, both, [2])

        last = ROUNDS - 1
        multiply_round(last, [0])
        add_b1(0)
        multiply_round(last, [1], [0])
        transpose_h(0)
        quantise_h(0)
        multiply_round(last, [1], [2])
        add_b1(1)
        transpose_h(1)
        multiply_h(0)
        quantise_h(1)
        multiply_h(1)

        v = tail.tile([P, B_TILES, M], F32)
        sums = tail.tile([P, B_TILES, 2], F32)
        clamped = tail.tile([P, B_TILES], F32)
        inv_norm = tail.tile([P, B_TILES], F32)
        unit_rows = tail.tile([P, B_TILES, M], F32)
        column_halves = [slice(0, M // 2), slice(M // 2, M)]
        for bt in range(B_TILES):
            for c, columns in enumerate(column_halves):
                nc.vector.tensor_tensor(
                    out=v[:, bt, columns],
                    in0=v_acc[bt][:, columns],
                    in1=b2_spread[:, columns],
                    op=ALU.add,
                )
                nc.scalar.activation(
                    out=unit_rows[:, bt, columns],
                    in_=v[:, bt, columns],
                    func=ACT.Square,
                    accum_out=sums[:, bt, c : c + 1],
                )
        for bt in range(B_TILES):
            nc.vector.tensor_scalar(
                out=clamped[:, bt : bt + 1],
                in0=sums[:, bt, 0:1],
                scalar1=sums[:, bt, 1:2],
                scalar2=EPS * EPS,
                op0=ALU.add,
                op1=ALU.max,
            )
            nc.scalar.activation(
                out=inv_norm[:, bt : bt + 1],
                in_=clamped[:, bt : bt + 1],
                func=ACT.Abs_reciprocal_sqrt,
            )
        for bt in range(B_TILES):
            nc.vector.tensor_scalar_mul(
                out=unit_rows[:, bt, column_halves[0]],
                in0=v[:, bt, column_halves[0]],
                scalar1=inv_norm[:, bt : bt + 1],
            )
            nc.scalar.activation(
                out=unit_rows[:, bt, column_halves[1]],
                in_=v[:, bt, column_halves[1]],
                func=ACT.Copy,
                scale=inv_norm[:, bt : bt + 1],
            )
            nc.sync.dma_start(out=out[bt * P : (bt + 1) * P, :], in_=unit_rows[:, bt])
